import numpy as np
import ml_dtypes


def mxq(x, axis, fmt="e4m3"):
    dtype, down = {"e4m3": (ml_dtypes.float8_e4m3fn, 7), "e5m2": (ml_dtypes.float8_e5m2, 14)}[fmt]
    v = np.moveaxis(np.asarray(x, np.float32).astype(ml_dtypes.bfloat16).astype(np.float64), axis, -1)
    blocks = v.reshape(v.shape[:-1] + (-1, 32))
    amax = np.abs(blocks).max(-1, keepdims=True)
    byte = np.maximum(np.where(amax > 0, np.frexp(amax)[1] - 1 + 127, 0) - down, 1)
    scale = np.exp2(byte - 127.0)
    codes = (blocks / scale).astype(np.float32).astype(dtype).astype(np.float64)
    return np.moveaxis((codes * scale).reshape(v.shape), -1, axis)


WIDE = False


def mx_kscale(k):
    if not WIDE:
        return np.ones(k)
    levels = np.array([10, -10, 5, -5, 0])
    if k % 512:
        return np.exp2(np.random.permutation(np.resize(levels, k // 32))).repeat(32)
    a = np.empty((k // 512, 16))
    for p in range(k // 512):
        a[p, :8] = np.random.permutation(np.resize(levels, 8))
        for g in range(8):
            far = levels[np.abs(levels - a[p, g]) >= 10]
            a[p, g + 8] = far[np.random.randint(len(far))]
    return np.exp2(a.ravel()).repeat(32)


BF16 = ml_dtypes.bfloat16


def bf(x):
    return np.asarray(x, np.float32).astype(BF16)


def f64(x):
    return np.asarray(x).astype(np.float64)


SQ, B, H, NP, HN, MQG = 512, 1, 2048, 16, 128, 2
ROT = HN // 2
QD, KVD = NP * HN, MQG * HN
QKV = QD + 2 * KVD
ROPE_BASE = 10000.0


def apply_rope(x, rope):
    sq, b, nh, hn = x.shape
    rot = rope.shape[-2] * 2
    xr, xp = x[..., :rot], x[..., rot:]
    xs = xr.reshape(sq, b, nh, rot // 2, 2)
    rc = rope[:sq].reshape(sq, -1, 1, rot // 2, 2)
    o0 = xs[..., 0] * rc[..., 0] - xs[..., 1] * rc[..., 1]
    o1 = xs[..., 1] * rc[..., 0] + xs[..., 0] * rc[..., 1]
    rotated = np.stack([o0, o1], -1).reshape(sq, b, nh, rot)
    return np.concatenate([rotated, xp], axis=-1)


def draw0():
    s = mx_kscale(H)
    pos = np.arange(SQ, dtype=np.float64)
    inv = 1.0 / (ROPE_BASE ** (np.arange(0, ROT, 2, dtype=np.float64) / ROT))
    ang = pos[:, None] * inv[None, :]
    rope = np.stack([np.cos(ang), np.sin(ang)], -1)[:, None, :, :]
    return {"hidden_states": bf(np.random.standard_normal((SQ, B, H)) * s),
            "Wqkv": bf(np.random.standard_normal((QKV, H)) * 1.3 / np.sqrt(H) / s[None, :]),
            "bqkv": bf(np.random.standard_normal(QKV) * 0.3),
            "rotary_pos_emb": bf(rope)}


def core(hidden_states, Wqkv, bqkv, rotary_pos_emb):
    x = f64(hidden_states)
    rope = f64(rotary_pos_emb)
    sq, b, _ = x.shape
    mixed = (mxq(x, 2, "e4m3") @ mxq(f64(Wqkv), 1, "e4m3").T) + f64(bqkv)
    q = mixed[..., :QD].reshape(sq, b, NP, HN)
    k = mixed[..., QD:QD + KVD].reshape(sq, b, MQG, HN)
    v = mixed[..., QD + KVD:].reshape(sq, b, MQG, HN)
    return apply_rope(q, rope), apply_rope(k, rope), v


def e4m3fn_bytes(y):
    return np.clip(np.asarray(y, np.float64), -448.0, 448.0).astype(np.float32).astype(ml_dtypes.float8_e4m3fn).view(np.uint8)


def e4m3fn_values(b):
    return np.asarray(b, np.uint8).view(ml_dtypes.float8_e4m3fn).astype(np.float64)


def setup_inputs():
    d = draw0()
    x0 = np.asarray(d['Wqkv']).astype(np.float64)
    s = (np.max(np.abs(x0), axis=(0,), keepdims=True) / 448.0).astype(np.float32)
    out = {}
    for k, v in d.items():
        if k == 'Wqkv':
            out['Wqkv_bytes'] = e4m3fn_bytes(x0 / s.astype(np.float64))
            out['Wqkv_scale'] = s
        else:
            out[k] = v
    return out


def reference(hidden_states, Wqkv_bytes, Wqkv_scale, bqkv, rotary_pos_emb):
    return core(hidden_states, e4m3fn_values(Wqkv_bytes) * Wqkv_scale.astype(np.float64), bqkv, rotary_pos_emb)

@@ -1,0 +1,375 @@
+from contextlib import ExitStack
+
+import concourse.mybir as mybir
+from concourse.masks import make_identity
+
+FLOPS = 2 * 512 * 2560 * 2048
+
+F32 = mybir.dt.float32
+BF16 = mybir.dt.bfloat16
+U32 = mybir.dt.uint32
+U8 = mybir.dt.uint8
+FP8 = mybir.dt.float8_e4m3fn
+FP8X4 = mybir.dt.float8_e4m3fn_x4
+ALU = mybir.AluOpType
+ACT = mybir.ActivationFunctionType
+
+P = 128
+K = 2048
+G = 4
+TOK = 512
+A = 4
+NPAIR = 10
+ROPE_PAIRS = 9
+MANUAL = True
+SEQ = [9, 0, 1, 2, 3, 4, 5, 6, 7, 8]
+
+
+def tile_selfattention_pa_kernel(
+    tc, hidden_states, Wqkv_bytes, Wqkv_scale, bqkv, rotary_pos_emb, out_0, out_1, out_2
+):
+    nc = tc.nc
+    with ExitStack() as ctx:
+        const = ctx.enter_context(tc.tile_pool(name="const", bufs=1))
+        wbp = ctx.enter_context(tc.tile_pool(name="wbp", bufs=3))
+        grpp = ctx.enter_context(tc.tile_pool(name="grpp", bufs=3))
+        wqp = ctx.enter_context(tc.tile_pool(name="wqp", bufs=2))
+        mp = ctx.enter_context(tc.tile_pool(name="mp", bufs=2))
+        ap_ = ctx.enter_context(tc.tile_pool(name="ap", bufs=3))
+        otp = ctx.enter_context(tc.tile_pool(name="otp", bufs=3))
+        pfp = ctx.enter_context(tc.psum_pool(name="pfp", bufs=3))
+        accp = ctx.enter_context(tc.psum_pool(name="accp", bufs=3))
+        pbp = ctx.enter_context(tc.psum_pool(name="pbp", bufs=2))
+        if MANUAL:
+            ctx.enter_context(tc.manual_schedule())
+
+        sc = const.tile([P, 2, K], F32, name="sc")
+        sflat = Wqkv_scale.rearrange("o k -> (o k)")
+        wby = {}
+        for i in SEQ:
+            wbytes = const.tile([P, 2, K], U8, name="wbytes%d" % i)
+            wby[i] = wbytes
+
+        def load_sc(c):
+            nc.sync.dma_start(
+                out=sc[:, 0, c * 512 : (c + 1) * 512],
+                in_=sflat[c * 512 : (c + 1) * 512].partition_broadcast(P),
+            )
+
+        def load_w(i, h0, h1):
+            nc.sync.dma_start(
+                out=wby[i][:, h0:h1, :],
+                in_=Wqkv_bytes[i * 256 + h0 * P : i * 256 + h1 * P, :].rearrange("(h p) k -> p h k", p=P),
+            )
+
+        load_sc(0)
+        load_w(SEQ[0], 0, 1)
+        load_sc(1)
+        load_sc(2)
+        load_sc(3)
+        load_w(SEQ[0], 1, 2)
+        load_w(SEQ[1], 0, 2)
+        xv = hidden_states.rearrange("(a p) o k -> a p (o k)", p=P)
+        xraw = []
+        for a in range(A):
+            xr = const.tile([P, K], BF16, name="xraw%d" % a)
+            nc.sync.dma_start(out=xr[:], in_=xv[a])
+            xraw.append(xr)
+        for i in SEQ[2:]:
+            load_w(i, 0, 2)
+
+        rraw = const.tile([P, A, 64], BF16, name="rraw")
+        nc.scalar.dma_start(out=rraw[:], in_=rotary_pos_emb.rearrange("(a p) o j c -> p a (o j c)", p=P))
+        bias_bf = const.tile([P, 2, 16], BF16, name="bias_bf")
+        bv = bqkv.rearrange("(i h x f) -> h f i x", h=2, x=2, f=64)
+        with nc.allow_non_contiguous_dma(reason="bias: one element to a partition"):
+            for h in range(2):
+                for x in range(2):
+                    nc.scalar.dma_start(
+                        out=bias_bf[h * 64 : (h + 1) * 64, x, 0:NPAIR],
+                        in_=bv[h][:, :, x],
+                    )
+
+        ident = const.tile([P, P], F32, name="ident")
+        make_identity(nc, ident[:])
+        pswap = const.tile([P, P], F32, name="pswap")
+        iv = ident[:].rearrange("p (j e) -> p j e", e=2)
+        pv = pswap[:].rearrange("p (j e) -> p j e", e=2)
+        nc.gpsimd.tensor_copy(out=pv[:, :, 0], in_=iv[:, :, 1])
+        nc.gpsimd.tensor_copy(out=pv[:, :, 1], in_=iv[:, :, 0])
+
+        tt = const.tile([P, 2 * A * P], F32, name="tt")
+        ttv = tt[:].rearrange("p (q a h j e) -> p q a h j e", q=2, a=A, h=2, e=2)
+        rv = rraw[:].rearrange("p a (j c) -> p a j c", c=2)
+        for e in range(2):
+            nc.scalar.activation(
+                out=ttv[:, 0, :, :, :, e],
+                in_=rv[:, :, :, 0].unsqueeze(2).to_broadcast([P, A, 2, 32]),
+                func=ACT.Copy,
+            )
+            nc.scalar.activation(
+                out=ttv[:, 1, :, :, :, e],
+                in_=rv[:, :, :, 1].unsqueeze(2).to_broadcast([P, A, 2, 32]),
+                func=ACT.Copy,
+                scale=(1.0 if e == 0 else -1.0),
+            )
+        cs = const.tile([P, 2, TOK], F32, name="cs")
+        for q in range(2):
+            ptab = pbp.tile([P, TOK], F32, name="ptab", tag="pb")
+            for a in range(A):
+                nc.tensor.transpose(
+                    out=ptab[:, a * P : (a + 1) * P],
+                    in_=tt[:, (q * A + a) * P : (q * A + a + 1) * P],
+                    identity=ident[:],
+                )
+            nc.scalar.copy(out=cs[:, q, :], in_=ptab[:])
+
+        bias = const.tile([P, 2, NPAIR], F32, name="bias")
+
+        xg = const.tile([P, G * TOK * 4], BF16, name="xg", align_bytes=64)
+        xgw = xg[:].bitcast(F32).rearrange("p (g n u) -> p g n u", g=G, u=2)
+        xq = const.tile([P, G * TOK], U32, name="xq", align_bytes=64)
+        xs = const.tile([P, G * TOK], U8, name="xs", align_bytes=64)
+
+        st = {}
+
+        def transposes(words, g0, g1):
+            banks = []
+            for gb in range(g0, g1, 2):
+                ng = min(2, g1 - gb)
+                pf = pfp.tile([P, 512], F32, name="pf", tag="pf")
+                for c in range(2 * ng):
+                    g = gb + c // 2
+                    u = c % 2
+                    nc.tensor.transpose(
+                        out=pf[:, c * P : (c + 1) * P],
+                        in_=words[:, 256 * g + u : 256 * (g + 1) : 2],
+                        identity=ident[:],
+                    )
+                banks.append((pf, gb, ng))
+            return banks
+
+        def x_turn(a):
+            for pf, gb, ng in transposes(xraw[a][:].bitcast(F32), 0, G):
+                nc.scalar.copy(
+                    out=xgw[:, gb : gb + ng, a * P : (a + 1) * P, :],
+                    in_=pf[:, 0 : ng * 256].rearrange("p (g u r) -> p g r u", g=ng, u=2),
+                )
+
+        def x_quant(g):
+            nc.vector.quantize_mx(
+                out=xq[:, g * TOK : (g + 1) * TOK].bitcast(FP8X4),
+                scales=xs[:, g * TOK : (g + 1) * TOK],
+                in_=xg[:, g * TOK * 4 : (g + 1) * TOK * 4],
+            )
+
+        def sc_copy(g0, g1):
+            cols = slice(g0 * 512, g1 * 512)
+            nc.scalar.copy(out=sc[:, 1, cols], in_=sc[:, 0, cols])
+
+        def wb_tile(i):
+            if ("wb", i) not in st:
+                wb = wbp.tile([P, 2, K], BF16, name="wb", tag="wb")
+                st[("wb", i)] = wb
+            return st[("wb", i)]
+
+        def widen(i, h, g0=0, g1=G):
+            wb = wb_tile(i)
+            cols = slice(g0 * 512, g1 * 512)
+            nc.vector.tensor_tensor(
+                out=wb[:, h, cols], in0=wby[i][:, h, cols].bitcast(FP8), in1=sc[:, 0, cols], op=ALU.mult
+            )
+
+        def widen2(i):
+            wb = wb_tile(i)
+            nc.vector.tensor_tensor(
+                out=wb[:].rearrange("p h k -> p (h k)"),
+                in0=wby[i][:].rearrange("p h k -> p (h k)").bitcast(FP8),
+                in1=sc[:].rearrange("p h k -> p (h k)"),
+                op=ALU.mult,
+            )
+
+        def w_turn(i, h, g0=0, g1=G):
+            if h == 0 and g0 == 0:
+                grp = grpp.tile([P, 2 * K], BF16, name="grp", tag="grp", align_bytes=64)
+                st[("grp", i)] = grp
+            grp = st[("grp", i)]
+            grpw = grp[:].bitcast(F32).rearrange("p (g x h f u) -> p g x h f u", g=G, x=2, h=2, u=2)
+            for pf, gb, ng in transposes(st[("wb", i)][:, h, :].bitcast(F32), g0, g1):
+                nc.scalar.copy(
+                    out=grpw[:, gb : gb + ng, :, h, :, :],
+                    in_=pf[:, 0 : ng * 256].rearrange("p (g u x f) -> p g x f u", g=ng, u=2, x=2),
+                )
+
+        def w_quant(i, g0=0, g1=G):
+            if g0 == 0:
+                wq = wqp.tile([P, 2 * TOK], U32, name="wq", tag="wq", align_bytes=64)
+                ws = wqp.tile([P, 2 * TOK], U8, name="ws", tag="ws", align_bytes=64)
+                st[("wq", i)] = (wq, ws)
+            wq, ws = st[("wq", i)]
+            nc.vector.quantize_mx(
+                out=wq[:, g0 * 256 : g1 * 256].bitcast(FP8X4),
+                scales=ws[:, g0 * 256 : g1 * 256],
+                in_=st[("grp", i)][:, g0 * 1024 : g1 * 1024],
+            )
+
+        def mm(i, x, g0=0, g1=G, spare=False):
+            wq, ws = st[("wq", i)]
+            if g0 == 0:
+                if spare:
+                    acc = pfp.tile([P, TOK], F32, name="acc2", tag="pf")
+                else:
+                    acc = accp.tile([P, TOK], F32, name="acc", tag="acc")
+                st[("acc", i, x)] = acc
+            acc = st[("acc", i, x)]
+            for g in range(g0, g1):
+                c0 = (g * 2 + x) * P
+                nc.tensor.matmul_mx(
+                    out=acc[:],
+                    lhsT=wq[:, c0 : c0 + P].bitcast(FP8X4),
+                    lhsT_scale=ws[:, c0 : c0 + P],
+                    rhs=xq[:, g * TOK : (g + 1) * TOK].bitcast(FP8X4),
+                    rhs_scale=xs[:, g * TOK : (g + 1) * TOK],
+                    start=(g == 0),
+                    stop=(g == G - 1),
+                )
+
+        def is_rope(i, x):
+            return x == 0 and i < ROPE_PAIRS
+
+        def leave_acc(i, x, a0=0, a1=A):
+            acc = st[("acc", i, x)]
+            col = bias[:, x, i : i + 1]
+            cols = slice(a0 * P, a1 * P)
+            if is_rope(i, x):
+                if a0 == 0:
+                    m = mp.tile([P, 2, TOK], F32, name="m", tag="m")
+                    st[("m", i, x)] = m
+                m = st[("m", i, x)]
+                nc.vector.scalar_tensor_tensor(
+                    out=m[:, :, cols],
+                    in0=acc[:, cols].unsqueeze(1).to_broadcast([P, 2, (a1 - a0) * P]),
+                    scalar=col,
+                    in1=cs[:, :, cols],
+                    op0=ALU.add,
+                    op1=ALU.mult,
+                )
+            else:
+                av = ap_.tile([P, TOK], F32, name="av", tag="av")
+                nc.scalar.activation(out=av[:], in_=acc[:], func=ACT.Identity, bias=col, scale=1.0)
+                st[("m", i, x)] = av
+
+        def back(i, x, a0=0, a1=A):
+            if ("ot", i) not in st:
+                ot = otp.tile([P, A, 2, P], F32, name="ot", tag="ot")
+                st[("ot", i)] = ot
+            ot = st[("ot", i)]
+            m = st[("m", i, x)]
+            if a0 == 0:
+                pb = pbp.tile([P, TOK], F32, name="pb", tag="pb")
+                st[("pb", i, x)] = pb
+            pb = st[("pb", i, x)]
+            for a in range(a0, a1):
+                blk = slice(a * P, (a + 1) * P)
+                if is_rope(i, x):
+                    nc.tensor.matmul(
+                        out=pb[:, blk], lhsT=m[:, 0, blk], rhs=ident[:], is_transpose=True, start=True, stop=False
+                    )
+                    nc.tensor.matmul(
+                        out=pb[:, blk], lhsT=m[:, 1, blk], rhs=pswap[:], is_transpose=True, start=False, stop=True
+                    )
+                else:
+                    nc.tensor.transpose(out=pb[:, blk], in_=m[:, blk], identity=ident[:])
+            nc.scalar.copy(
+                out=ot[:, a0:a1, :, x * 64 : (x + 1) * 64],
+                in_=pb[:, a0 * P : a1 * P].rearrange("p (a h f) -> p a h f", a=a1 - a0, h=2),
+            )
+
+        def store(i, a0=0, a1=A):
+            if i < 8:
+                dst = out_0.rearrange("(a p) o h f -> p a (o h) f", p=P)[:, :, 2 * i : 2 * i + 2, :]
+            elif i == 8:
+                dst = out_1.rearrange("(a p) o h f -> p a (o h) f", p=P)
+            else:
+                dst = out_2.rearrange("(a p) o h f -> p a (o h) f", p=P)
+            nc.sync.dma_start(out=dst[:, a0:a1], in_=st[("ot", i)][:, a0:a1])
+
+        s0, s1, s2 = SEQ[0], SEQ[1], SEQ[2]
+        for c in range(G):
+            widen(s0, 0, c, c + 1)
+        widen(s0, 1)
+        w_turn(s0, 0)
+        sc_copy(0, 2)
+        sc_copy(2, 4)
+        w_turn(s0, 1)
+        widen(s1, 0)
+        widen(s1, 1)
+        for a in range(A):
+            x_turn(a)
+        w_turn(s1, 0)
+        w_turn(s1, 1)
+        w_quant(s0)
+        widen2(s2)
+        nc.vector.tensor_copy(out=bias[:], in_=bias_bf[:, :, 0:NPAIR])
+        for g in range(G):
+            x_quant(g)
+        mm(s0, 1, 0, 2)
+        mm(s0, 0, 0, 2)
+        mm(s0, 1, 2, 4)
+        leave_acc(s0, 1)
+        mm(s0, 0, 2, 4)
+        leave_acc(s0, 0)
+        w_turn(s2, 0)
+        w_quant(s1)
+        mm(s1, 0, 0, 2)
+        for n in range(3, NPAIR - 1):
+            cur, p1, p2, p3 = SEQ[n], SEQ[n - 1], SEQ[n - 2], SEQ[n - 3]
+            widen2(cur)
+            w_turn(p1, 1)
+            mm(p2, 0, 2, 4)
+            back(p3, 0)
+            mm(p2, 1, 0, 2)
+            w_turn(cur, 0)
+            mm(p2, 1, 2, 4)
+            leave_acc(p2, 1)
+            back(p3, 1)
+            store(p3)
+            w_quant(p1)
+            leave_acc(p2, 0)
+            mm(p1, 0, 0, 2)
+        cur, p1, p2, p3 = SEQ[9], SEQ[8], SEQ[7], SEQ[6]
+        widen(cur, 0)
+        w_turn(p1, 1)
+        back(p3, 1)
+        back(p3, 0)
+        widen(cur, 1)
+        w_turn(cur, 0)
+        mm(p2, 1, 0, 2)
+        store(p3)
+        mm(p2, 1, 2, 4)
+        leave_acc(p2, 1)
+        mm(p2, 0, 2, 4)
+        w_turn(cur, 1)
+        w_quant(p1)
+        back(p2, 1)
+        mm(p1, 0)
+        leave_acc(p2, 0)
+        back(p2, 0)
+        mm(p1, 1)
+        w_quant(cur)
+        leave_acc(p1, 1)
+        leave_acc(p1, 0)
+        mm(cur, 1)
+        mm(cur, 0)
+        leave_acc(cur, 1)
+        back(p1, 1)
+        leave_acc(cur, 0, 0, 2)
+        back(p1, 0)
+        leave_acc(cur, 0, 2, 4)
+        back(cur, 1)
+        back(cur, 0, 0, 2)
+        store(p2)
+        back(cur, 0, 2, 4)
+        store(p1)
+        store(cur, 0, 2)
+        store(cur, 2, 4)

@@ -326,14 +326,14 @@ def tile_selfattention_pa_kernel(
             cur, p1, p2, p3 = SEQ[n], SEQ[n - 1], SEQ[n - 2], SEQ[n - 3]
             widen2(cur)
             w_turn(p1, 1)
-            mm(p2, 0, 2, 4)
             back(p3, 0)
+            mm(p2, 0, 2, 4)
             mm(p2, 1, 0, 2)
             w_turn(cur, 0)
-            mm(p2, 1, 2, 4)
-            leave_acc(p2, 1)
             back(p3, 1)
             store(p3)
+            mm(p2, 1, 2, 4)
+            leave_acc(p2, 1)
             w_quant(p1)
             leave_acc(p2, 0)
             mm(p1, 0, 0, 2)

@@ -77,6 +77,8 @@ def tile_selfattention_pa_kernel(
             xraw.append(xr)
         for i in SEQ[2:]:
             load_w(i, 0, 2)
+        scol = const.tile([P, G, 4], F32, name="scol")
+        nc.sync.dma_start(out=scol[:], in_=Wqkv_scale.rearrange("o (g p t) -> p (o g) t", p=P, t=4))
 
         rraw = const.tile([P, A, 64], BF16, name="rraw")
         nc.scalar.dma_start(out=rraw[:], in_=rotary_pos_emb.rearrange("(a p) o j c -> p a (o j c)", p=P))
@@ -114,15 +116,17 @@ def tile_selfattention_pa_kernel(
                 scale=(1.0 if e == 0 else -1.0),
             )
         cs = const.tile([P, 2, TOK], F32, name="cs")
-        for q in range(2):
-            ptab = pbp.tile([P, TOK], F32, name="ptab", tag="pb")
-            for a in range(A):
-                nc.tensor.transpose(
-                    out=ptab[:, a * P : (a + 1) * P],
-                    in_=tt[:, (q * A + a) * P : (q * A + a + 1) * P],
-                    identity=ident[:],
-                )
-            nc.scalar.copy(out=cs[:, q, :], in_=ptab[:])
+
+        def tables_turn():
+            for q in range(2):
+                ptab = pbp.tile([P, TOK], F32, name="ptab", tag="pb")
+                for a in range(A):
+                    nc.tensor.transpose(
+                        out=ptab[:, a * P : (a + 1) * P],
+                        in_=tt[:, (q * A + a) * P : (q * A + a + 1) * P],
+                        identity=ident[:],
+                    )
+                nc.scalar.copy(out=cs[:, q, :], in_=ptab[:])
 
         bias = const.tile([P, 2, NPAIR], F32, name="bias")
 
@@ -156,11 +160,11 @@ def tile_selfattention_pa_kernel(
                     in_=pf[:, 0 : ng * 256].rearrange("p (g u r) -> p g r u", g=ng, u=2),
                 )
 
-        def x_quant(g):
+        def x_quant(g0, g1):
             nc.vector.quantize_mx(
-                out=xq[:, g * TOK : (g + 1) * TOK].bitcast(FP8X4),
-                scales=xs[:, g * TOK : (g + 1) * TOK],
-                in_=xg[:, g * TOK * 4 : (g + 1) * TOK * 4],
+                out=xq[:, g0 * TOK : g1 * TOK].bitcast(FP8X4),
+                scales=xs[:, g0 * TOK : g1 * TOK],
+                in_=xg[:, g0 * TOK * 4 : g1 * TOK * 4],
             )
 
         def sc_copy(g0, g1):
@@ -234,6 +238,45 @@ def tile_selfattention_pa_kernel(
                     stop=(g == G - 1),
                 )
 
+        SP = SEQ[NPAIR - 1]
+        wc = const.tile([P, 2, K], BF16, name="wc")
+        spw = const.tile([P, G, 2, 256, 2], BF16, name="spw")
+        grp_sp = const.tile([P, 2 * K], BF16, name="grp_sp", align_bytes=64)
+        st[("grp", SP)] = grp_sp
+
+        def sp_cast(h, g0, g1):
+            cols = slice(g0 * 512, g1 * 512)
+            nc.scalar.copy(out=wc[:, h, cols], in_=wby[SP][:, h, cols].bitcast(FP8))
+
+        def sp_turn(g):
+            pf = pfp.tile([P, 512], F32, name="pf", tag="pf")
+            st[("spf", g)] = pf
+            for h in range(2):
+                for u in range(2):
+                    c = 2 * h + u
+                    nc.tensor.transpose(
+                        out=pf[:, c * P : (c + 1) * P],
+                        in_=wc[:, h, :].bitcast(F32)[:, 256 * g + u : 256 * (g + 1) : 2],
+                        identity=ident[:],
+                    )
+
+        def sp_scale(g):
+            pfb = st[("spf", g)][:].bitcast(BF16).rearrange("p (h u x f e) -> p h u x f e", h=2, u=2, x=2, e=2)
+            for u in range(2):
+                for e in range(2):
+                    nc.scalar.activation(
+                        out=spw[:, g, u, :, e].rearrange("p (x h f) -> p h x f", x=2, h=2),
+                        in_=pfb[:, :, u, :, :, e],
+                        func=ACT.Copy,
+                        scale=scol[:, g, 2 * u + e : 2 * u + e + 1],
+                    )
+
+        def sp_weave(g):
+            nc.scalar.copy(
+                out=grp_sp[:].bitcast(F32).rearrange("p (g c u) -> p g c u", g=G, u=2)[:, g],
+                in_=spw[:, g].rearrange("p u c e -> p u (c e)").bitcast(F32).rearrange("p u c -> p c u"),
+            )
+
         def is_rope(i, x):
             return x == 0 and i < ROPE_PAIRS
 
@@ -302,6 +345,7 @@ def tile_selfattention_pa_kernel(
         sc_copy(0, 2)
         sc_copy(2, 4)
         w_turn(s0, 1)
+        tables_turn()
         widen(s1, 0)
         widen(s1, 1)
         for a in range(A):
@@ -311,8 +355,8 @@ def tile_selfattention_pa_kernel(
         w_quant(s0)
         widen2(s2)
         nc.vector.tensor_copy(out=bias[:], in_=bias_bf[:, :, 0:NPAIR])
-        for g in range(G):
-            x_quant(g)
+        x_quant(0, 2)
+        x_quant(2, 4)
         mm(s0, 1, 0, 2)
         mm(s0, 0, 0, 2)
         mm(s0, 1, 2, 4)
@@ -322,54 +366,58 @@ def tile_selfattention_pa_kernel(
         w_turn(s2, 0)
         w_quant(s1)
         mm(s1, 0, 0, 2)
+        slot1 = {0: [(sp_cast, (0, 0, 2))], 1: [(sp_scale, (0,))], 2: [(sp_scale, (1,))], 3: [(sp_cast, (0, 2, 4))], 4: [(sp_scale, (2,))], 5: [(sp_scale, (3,))]}
+        slot2 = {0: [(sp_cast, (1, 0, 2))], 1: [(sp_weave, (0,))], 2: [(sp_weave, (1,))], 3: [(sp_cast, (1, 2, 4))], 4: [(sp_weave, (2,))], 5: [(sp_weave, (3,))]}
+        turn = {1: 0, 2: 1, 4: 2, 5: 3}
         for n in range(3, NPAIR - 1):
             cur, p1, p2, p3 = SEQ[n], SEQ[n - 1], SEQ[n - 2], SEQ[n - 3]
+            k = n - 3
             widen2(cur)
             w_turn(p1, 1)
+            if k in turn:
+                sp_turn(turn[k])
             back(p3, 0)
+            for f, a in slot1[k]:
+                f(*a)
             mm(p2, 0, 2, 4)
-            mm(p2, 1, 0, 2)
-            w_turn(cur, 0)
+            mm(p2, 1)
+            leave_acc(p2, 1)
             back(p3, 1)
             store(p3)
-            mm(p2, 1, 2, 4)
-            leave_acc(p2, 1)
+            w_turn(cur, 0)
+            for f, a in slot2[k]:
+                f(*a)
             w_quant(p1)
             leave_acc(p2, 0)
             mm(p1, 0, 0, 2)
-        cur, p1, p2, p3 = SEQ[9], SEQ[8], SEQ[7], SEQ[6]
-        widen(cur, 0)
-        w_turn(p1, 1)
-        back(p3, 1)
-        back(p3, 0)
-        widen(cur, 1)
-        w_turn(cur, 0)
-        mm(p2, 1, 0, 2)
-        store(p3)
-        mm(p2, 1, 2, 4)
-        leave_acc(p2, 1)
-        mm(p2, 0, 2, 4)
-        w_turn(cur, 1)
-        w_quant(p1)
-        back(p2, 1)
-        mm(p1, 0)
-        leave_acc(p2, 0)
-        back(p2, 0)
-        mm(p1, 1)
-        w_quant(cur)
-        leave_acc(p1, 1)
-        leave_acc(p1, 0)
-        mm(cur, 1)
-        mm(cur, 0)
-        leave_acc(cur, 1)
-        back(p1, 1)
-        leave_acc(cur, 0, 0, 2)
-        back(p1, 0)
-        leave_acc(cur, 0, 2, 4)
-        back(cur, 1)
-        back(cur, 0, 0, 2)
-        store(p2)
-        back(cur, 0, 2, 4)
-        store(p1)
-        store(cur, 0, 2)
-        store(cur, 2, 4)
+        C, B, A_, Z = SEQ[9], SEQ[8], SEQ[7], SEQ[6]
+        w_turn(B, 1)
+        w_quant(C)
+        mm(A_, 0, 2, 4)
+        mm(A_, 1)
+        leave_acc(A_, 1)
+        back(Z, 0)
+        back(Z, 1)
+        store(Z)
+        leave_acc(A_, 0)
+        w_quant(B)
+        mm(C, 0)
+        mm(C, 1)
+        leave_acc(C, 1)
+        leave_acc(C, 0)
+        back(A_, 1)
+        back(A_, 0)
+        store(A_)
+        mm(B, 0)
+        mm(B, 1)
+        leave_acc(B, 0, 0, 2)
+        leave_acc(B, 1)
+        leave_acc(B, 0, 2, 4)
+        back(C, 1)
+        back(C, 0)
+        store(C)
+        back(B, 0, 0, 2)
+        back(B, 1)
+        store(B, 0, 2)
+        back(B, 0, 2, 4)
+        store(B, 2, 4)

@@ -75,22 +75,27 @@ def tile_selfattention_pa_kernel(
             xr = const.tile([P, K], BF16, name="xraw%d" % a)
             nc.sync.dma_start(out=xr[:], in_=xv[a])
             xraw.append(xr)
-        for i in SEQ[2:]:
+        for i in SEQ[2:4]:
+            load_w(i, 0, 2)
+        bias_bf = const.tile([P, 2, 16], BF16, name="bias_bf")
+        bv = bqkv.rearrange("(i h x f) -> h f i x", h=2, x=2, f=64)
+        with nc.allow_non_contiguous_dma(reason="bias: one element to a partition"):
+            for h in range(2):
+                for x in range(2):
+                    nc.sync.dma_start(
+                        out=bias_bf[h * 64 : (h + 1) * 64, x, 0:NPAIR],
+                        in_=bv[h][:, :, x],
+                    )
+        for i in SEQ[4:]:
             load_w(i, 0, 2)
         scol = const.tile([P, G, 4], F32, name="scol")
         nc.sync.dma_start(out=scol[:], in_=Wqkv_scale.rearrange("o (g p t) -> p (o g) t", p=P, t=4))
 
         rraw = const.tile([P, A, 64], BF16, name="rraw")
         nc.scalar.dma_start(out=rraw[:], in_=rotary_pos_emb.rearrange("(a p) o j c -> p a (o j c)", p=P))
-        bias_bf = const.tile([P, 2, 16], BF16, name="bias_bf")
-        bv = bqkv.rearrange("(i h x f) -> h f i x", h=2, x=2, f=64)
-        with nc.allow_non_contiguous_dma(reason="bias: one element to a partition"):
-            for h in range(2):
-                for x in range(2):
-                    nc.scalar.dma_start(
-                        out=bias_bf[h * 64 : (h + 1) * 64, x, 0:NPAIR],
-                        in_=bv[h][:, :, x],
-                    )
+        warm = const.tile([P, 2], F32, name="warm")
+        nc.vector.memset(warm[:, 0:1], 0.0)
+        nc.scalar.activation(out=warm[:, 1:2], in_=warm[:, 0:1], func=ACT.Copy)
 
         ident = const.tile([P, P], F32, name="ident")
         make_identity(nc, ident[:])
@@ -354,9 +359,9 @@ def tile_selfattention_pa_kernel(
         w_turn(s1, 1)
         w_quant(s0)
         widen2(s2)
-        nc.vector.tensor_copy(out=bias[:], in_=bias_bf[:, :, 0:NPAIR])
         x_quant(0, 2)
         x_quant(2, 4)
+        nc.vector.tensor_copy(out=bias[:], in_=bias_bf[:, :, 0:NPAIR])
         mm(s0, 1, 0, 2)
         mm(s0, 0, 0, 2)
         mm(s0, 1, 2, 4)

@@ -37,6 +37,7 @@ def tile_selfattention_pa_kernel(
         mp = ctx.enter_context(tc.tile_pool(name="mp", bufs=2))
         ap_ = ctx.enter_context(tc.tile_pool(name="ap", bufs=3))
         otp = ctx.enter_context(tc.tile_pool(name="otp", bufs=3))
+        rtp = ctx.enter_context(tc.tile_pool(name="rtp", bufs=2))
         pfp = ctx.enter_context(tc.psum_pool(name="pfp", bufs=3))
         accp = ctx.enter_context(tc.psum_pool(name="accp", bufs=3))
         pbp = ctx.enter_context(tc.psum_pool(name="pbp", bufs=2))
@@ -77,17 +78,22 @@ def tile_selfattention_pa_kernel(
             xraw.append(xr)
         for i in SEQ[2:4]:
             load_w(i, 0, 2)
-        bias_bf = const.tile([P, 2, 16], BF16, name="bias_bf")
-        bv = bqkv.rearrange("(i h x f) -> h f i x", h=2, x=2, f=64)
-        with nc.allow_non_contiguous_dma(reason="bias: one element to a partition"):
-            for h in range(2):
-                for x in range(2):
-                    nc.sync.dma_start(
-                        out=bias_bf[h * 64 : (h + 1) * 64, x, 0:NPAIR],
-                        in_=bv[h][:, :, x],
-                    )
+        brows = const.tile([P, P], BF16, name="brows")
+        nc.gpsimd.memset(brows[:], 0.0)
+        bv = bqkv.rearrange("(i h x f) -> x i h f", h=2, x=2, f=64)
+        for x in range(2):
+            nc.sync.dma_start(
+                out=brows[x * 16 : x * 16 + NPAIR, :].rearrange("i (h f) -> i h f", h=2),
+                in_=bv[x],
+            )
         for i in SEQ[4:]:
             load_w(i, 0, 2)
+        NAT = (SEQ[NPAIR - 1],)
+        brow = {}
+        for i in NAT:
+            br = const.tile([P, 256], BF16, name="brow%d" % i)
+            brow[i] = br
+            nc.sync.dma_start(out=br[:], in_=bqkv[i * 256 : (i + 1) * 256].partition_broadcast(P))
         scol = const.tile([P, G, 4], F32, name="scol")
         nc.sync.dma_start(out=scol[:], in_=Wqkv_scale.rearrange("o (g p t) -> p (o g) t", p=P, t=4))
 
@@ -104,6 +110,8 @@ def tile_selfattention_pa_kernel(
         pv = pswap[:].rearrange("p (j e) -> p j e", e=2)
         nc.gpsimd.tensor_copy(out=pv[:, :, 0], in_=iv[:, :, 1])
         nc.gpsimd.tensor_copy(out=pv[:, :, 1], in_=iv[:, :, 0])
+        identb = const.tile([P, P], BF16, name="identb")
+        make_identity(nc, identb[:])
 
         tt = const.tile([P, 2 * A * P], F32, name="tt")
         ttv = tt[:].rearrange("p (q a h j e) -> p q a h j e", q=2, a=A, h=2, e=2)
@@ -266,12 +274,12 @@ def tile_selfattention_pa_kernel(
                     )
 
         def sp_scale(g):
-            pfb = st[("spf", g)][:].bitcast(BF16).rearrange("p (h u x f e) -> p h u x f e", h=2, u=2, x=2, e=2)
+            pfb = st[("spf", g)][:].bitcast(BF16).rearrange("p (h u r e) -> p h u r e", h=2, u=2, e=2)
             for u in range(2):
                 for e in range(2):
                     nc.scalar.activation(
-                        out=spw[:, g, u, :, e].rearrange("p (x h f) -> p h x f", x=2, h=2),
-                        in_=pfb[:, :, u, :, :, e],
+                        out=spw[:, g, u, :, e].rearrange("p (h r) -> p h r", h=2),
+                        in_=pfb[:, :, u, :, e],
                         func=ACT.Copy,
                         scale=scol[:, g, 2 * u + e : 2 * u + e + 1],
                     )
@@ -281,6 +289,53 @@ def tile_selfattention_pa_kernel(
                 out=grp_sp[:].bitcast(F32).rearrange("p (g c u) -> p g c u", g=G, u=2)[:, g],
                 in_=spw[:, g].rearrange("p u c e -> p u (c e)").bitcast(F32).rearrange("p u c -> p c u"),
             )
+
+        def mm_tok(i, half):
+            wq, ws = st[("wq", i)]
+            acc = accp.tile([P, 2, 256], F32, name="acct", tag="acc")
+            st[("acct", i, half)] = acc
+            for a2 in range(2):
+                for g in range(G):
+                    c0 = g * TOK + (2 * half + a2) * P
+                    nc.tensor.matmul_mx(
+                        out=acc[:, a2, :],
+                        lhsT=xq[:, c0 : c0 + P].bitcast(FP8X4),
+                        lhsT_scale=xs[:, c0 : c0 + P],
+                        rhs=wq[:, g * 256 : (g + 1) * 256].bitcast(FP8X4),
+                        rhs_scale=ws[:, g * 256 : (g + 1) * 256],
+                        start=(g == 0),
+                        stop=(g == G - 1),
+                    )
+
+        def leave_tok(i, half):
+            if ("ot", i) not in st:
+                ot = otp.tile([P, A, 2, P], F32, name="ot", tag="ot")
+                st[("ot", i)] = ot
+            nc.vector.tensor_tensor(
+                out=st[("ot", i)][:, 2 * half : 2 * half + 2, :, :].rearrange("p a h f -> p a (h f)"),
+                in0=st[("acct", i, half)][:],
+                in1=brow[i][:].unsqueeze(1).to_broadcast([P, 2, 256]),
+                op=ALU.add,
+            )
+
+        ttq = tt[:].rearrange("p (q a h c) -> p q a h c", q=2, a=A, h=2)
+
+        def rope_tok(i, half, step):
+            rot = st[("ot", i)][:, 2 * half : 2 * half + 2, :, 0:64]
+            if step == 0:
+                t1 = rtp.tile([P, 2, 2, 64], F32, name="t1", tag="t1")
+                m1 = rtp.tile([P, 2, 2, 64], F32, name="m1", tag="m1")
+                st[("rt", i, half)] = (t1, m1)
+                nc.vector.tensor_tensor(out=t1[:], in0=rot, in1=ttq[:, 0, 2 * half : 2 * half + 2], op=ALU.mult)
+                nc.vector.tensor_tensor(
+                    out=m1[:].rearrange("p a h (j e) -> p (a h) j e", e=2),
+                    in0=rot.rearrange("p a h (j e) -> p (a h) j e", e=2)[:, :, :, ::-1],
+                    in1=ttq[:, 1, 2 * half : 2 * half + 2].rearrange("p a h (j e) -> p (a h) j e", e=2),
+                    op=ALU.mult,
+                )
+            else:
+                t1, m1 = st[("rt", i, half)]
+                nc.vector.tensor_tensor(out=rot, in0=t1[:], in1=m1[:], op=ALU.subtract)
 
         def is_rope(i, x):
             return x == 0 and i < ROPE_PAIRS
@@ -357,11 +412,13 @@ def tile_selfattention_pa_kernel(
             x_turn(a)
         w_turn(s1, 0)
         w_turn(s1, 1)
+        pbias = pbp.tile([P, P], BF16, name="pbias", tag="pb")
+        nc.tensor.transpose(out=pbias[:], in_=brows[:], identity=identb[:])
         w_quant(s0)
         widen2(s2)
         x_quant(0, 2)
         x_quant(2, 4)
-        nc.vector.tensor_copy(out=bias[:], in_=bias_bf[:, :, 0:NPAIR])
+        nc.vector.tensor_copy(out=bias[:], in_=pbias[:, 0:32].rearrange("p (x r) -> p x r", x=2)[:, :, 0:NPAIR])
         mm(s0, 1, 0, 2)
         mm(s0, 0, 0, 2)
         mm(s0, 1, 2, 4)
@@ -370,7 +427,6 @@ def tile_selfattention_pa_kernel(
         leave_acc(s0, 0)
         w_turn(s2, 0)
         w_quant(s1)
-        mm(s1, 0, 0, 2)
         slot1 = {0: [(sp_cast, (0, 0, 2))], 1: [(sp_scale, (0,))], 2: [(sp_scale, (1,))], 3: [(sp_cast, (0, 2, 4))], 4: [(sp_scale, (2,))], 5: [(sp_scale, (3,))]}
         slot2 = {0: [(sp_cast, (1, 0, 2))], 1: [(sp_weave, (0,))], 2: [(sp_weave, (1,))], 3: [(sp_cast, (1, 2, 4))], 4: [(sp_weave, (2,))], 5: [(sp_weave, (3,))]}
         turn = {1: 0, 2: 1, 4: 2, 5: 3}
@@ -379,50 +435,52 @@ def tile_selfattention_pa_kernel(
             k = n - 3
             widen2(cur)
             w_turn(p1, 1)
+            back(p3, 0)
             if k in turn:
                 sp_turn(turn[k])
-            back(p3, 0)
             for f, a in slot1[k]:
                 f(*a)
-            mm(p2, 0, 2, 4)
+            mm(p2, 0)
             mm(p2, 1)
             leave_acc(p2, 1)
+            w_turn(cur, 0)
             back(p3, 1)
             store(p3)
-            w_turn(cur, 0)
             for f, a in slot2[k]:
                 f(*a)
             w_quant(p1)
             leave_acc(p2, 0)
-            mm(p1, 0, 0, 2)
         C, B, A_, Z = SEQ[9], SEQ[8], SEQ[7], SEQ[6]
         w_turn(B, 1)
         w_quant(C)
-        mm(A_, 0, 2, 4)
+        mm(A_, 0)
         mm(A_, 1)
         leave_acc(A_, 1)
+        mm_tok(C, 0)
         back(Z, 0)
         back(Z, 1)
         store(Z)
         leave_acc(A_, 0)
         w_quant(B)
-        mm(C, 0)
-        mm(C, 1)
-        leave_acc(C, 1)
-        leave_acc(C, 0)
+        mm_tok(C, 1)
+        leave_tok(C, 0)
+        rope_tok(C, 0, 0)
         back(A_, 1)
         back(A_, 0)
         store(A_)
         mm(B, 0)
         mm(B, 1)
+        leave_tok(C, 1)
+        rope_tok(C, 0, 1)
+        store(C, 0, 2)
         leave_acc(B, 0, 0, 2)
         leave_acc(B, 1)
         leave_acc(B, 0, 2, 4)
-        back(C, 1)
-        back(C, 0)
-        store(C)
+        rope_tok(C, 1, 0)
         back(B, 0, 0, 2)
         back(B, 1)
         store(B, 0, 2)
         back(B, 0, 2, 4)
+        rope_tok(C, 1, 1)
+        store(C, 2, 4)
         store(B, 2, 4)

@@ -33,10 +33,10 @@ def tile_selfattention_pa_kernel(
         const = ctx.enter_context(tc.tile_pool(name="const", bufs=1))
         wbp = ctx.enter_context(tc.tile_pool(name="wbp", bufs=3))
         grpp = ctx.enter_context(tc.tile_pool(name="grpp", bufs=3))
-        wqp = ctx.enter_context(tc.tile_pool(name="wqp", bufs=2))
+        wqp = ctx.enter_context(tc.tile_pool(name="wqp", bufs=3))
         mp = ctx.enter_context(tc.tile_pool(name="mp", bufs=2))
         ap_ = ctx.enter_context(tc.tile_pool(name="ap", bufs=3))
-        otp = ctx.enter_context(tc.tile_pool(name="otp", bufs=3))
+        otp = ctx.enter_context(tc.tile_pool(name="otp", bufs=4))
         rtp = ctx.enter_context(tc.tile_pool(name="rtp", bufs=2))
         pfp = ctx.enter_context(tc.psum_pool(name="pfp", bufs=3))
         accp = ctx.enter_context(tc.psum_pool(name="accp", bufs=3))
@@ -78,6 +78,7 @@ def tile_selfattention_pa_kernel(
             xraw.append(xr)
         for i in SEQ[2:4]:
             load_w(i, 0, 2)
+        load_w(SEQ[NPAIR - 1], 0, 2)
         brows = const.tile([P, P], BF16, name="brows")
         nc.gpsimd.memset(brows[:], 0.0)
         bv = bqkv.rearrange("(i h x f) -> x i h f", h=2, x=2, f=64)
@@ -86,9 +87,9 @@ def tile_selfattention_pa_kernel(
                 out=brows[x * 16 : x * 16 + NPAIR, :].rearrange("i (h f) -> i h f", h=2),
                 in_=bv[x],
             )
-        for i in SEQ[4:]:
+        for i in SEQ[4 : NPAIR - 1]:
             load_w(i, 0, 2)
-        NAT = (SEQ[NPAIR - 1],)
+        NAT = (SEQ[NPAIR - 2], SEQ[NPAIR - 1])
         brow = {}
         for i in NAT:
             br = const.tile([P, 256], BF16, name="brow%d" % i)
@@ -212,11 +213,18 @@ def tile_selfattention_pa_kernel(
                 st[("grp", i)] = grp
             grp = st[("grp", i)]
             grpw = grp[:].bitcast(F32).rearrange("p (g x h f u) -> p g x h f u", g=G, x=2, h=2, u=2)
+            grpn = grp[:].bitcast(F32).rearrange("p (g h r u) -> p g h r u", g=G, h=2, u=2)
             for pf, gb, ng in transposes(st[("wb", i)][:, h, :].bitcast(F32), g0, g1):
-                nc.scalar.copy(
-                    out=grpw[:, gb : gb + ng, :, h, :, :],
-                    in_=pf[:, 0 : ng * 256].rearrange("p (g u x f) -> p g x f u", g=ng, u=2, x=2),
-                )
+                if i in NAT:
+                    nc.scalar.copy(
+                        out=grpn[:, gb : gb + ng, h, :, :],
+                        in_=pf[:, 0 : ng * 256].rearrange("p (g u r) -> p g r u", g=ng, u=2),
+                    )
+                else:
+                    nc.scalar.copy(
+                        out=grpw[:, gb : gb + ng, :, h, :, :],
+                        in_=pf[:, 0 : ng * 256].rearrange("p (g u x f) -> p g x f u", g=ng, u=2, x=2),
+                    )
 
         def w_quant(i, g0=0, g1=G):
             if g0 == 0:
@@ -414,6 +422,8 @@ def tile_selfattention_pa_kernel(
         w_turn(s1, 1)
         pbias = pbp.tile([P, P], BF16, name="pbias", tag="pb")
         nc.tensor.transpose(out=pbias[:], in_=brows[:], identity=identb[:])
+        sp_cast(0, 0, 2)
+        sp_cast(1, 0, 2)
         w_quant(s0)
         widen2(s2)
         x_quant(0, 2)
@@ -427,9 +437,9 @@ def tile_selfattention_pa_kernel(
         leave_acc(s0, 0)
         w_turn(s2, 0)
         w_quant(s1)
-        slot1 = {0: [(sp_cast, (0, 0, 2))], 1: [(sp_scale, (0,))], 2: [(sp_scale, (1,))], 3: [(sp_cast, (0, 2, 4))], 4: [(sp_scale, (2,))], 5: [(sp_scale, (3,))]}
-        slot2 = {0: [(sp_cast, (1, 0, 2))], 1: [(sp_weave, (0,))], 2: [(sp_weave, (1,))], 3: [(sp_cast, (1, 2, 4))], 4: [(sp_weave, (2,))], 5: [(sp_weave, (3,))]}
-        turn = {1: 0, 2: 1, 4: 2, 5: 3}
+        slot1 = {0: [(sp_scale, (0,))], 1: [(sp_scale, (1,))], 2: [(sp_cast, (0, 2, 4))], 3: [(sp_scale, (2,))], 4: [(sp_scale, (3,))], 5: []}
+        slot2 = {0: [(sp_weave, (0,))], 1: [(sp_weave, (1,))], 2: [(sp_cast, (1, 2, 4))], 3: [(sp_weave, (2,))], 4: [(sp_weave, (3,))], 5: []}
+        turn = {0: 0, 1: 1, 3: 2, 4: 3}
         for n in range(3, NPAIR - 1):
             cur, p1, p2, p3 = SEQ[n], SEQ[n - 1], SEQ[n - 2], SEQ[n - 3]
             k = n - 3
@@ -451,36 +461,36 @@ def tile_selfattention_pa_kernel(
             w_quant(p1)
             leave_acc(p2, 0)
         C, B, A_, Z = SEQ[9], SEQ[8], SEQ[7], SEQ[6]
+        mm(A_, 0)
         w_turn(B, 1)
         w_quant(C)
-        mm(A_, 0)
+        mm_tok(C, 0)
         mm(A_, 1)
         leave_acc(A_, 1)
-        mm_tok(C, 0)
+        leave_acc(A_, 0)
+        mm_tok(C, 1)
+        w_quant(B)
         back(Z, 0)
         back(Z, 1)
         store(Z)
-        leave_acc(A_, 0)
-        w_quant(B)
-        mm_tok(C, 1)
         leave_tok(C, 0)
         rope_tok(C, 0, 0)
-        back(A_, 1)
-        back(A_, 0)
-        store(A_)
-        mm(B, 0)
-        mm(B, 1)
+        mm_tok(B, 0)
         leave_tok(C, 1)
         rope_tok(C, 0, 1)
         store(C, 0, 2)
-        leave_acc(B, 0, 0, 2)
-        leave_acc(B, 1)
-        leave_acc(B, 0, 2, 4)
+        mm_tok(B, 1)
         rope_tok(C, 1, 0)
-        back(B, 0, 0, 2)
-        back(B, 1)
-        store(B, 0, 2)
-        back(B, 0, 2, 4)
+        back(A_, 1)
+        back(A_, 0)
+        store(A_)
+        leave_tok(B, 0)
         rope_tok(C, 1, 1)
         store(C, 2, 4)
+        rope_tok(B, 0, 0)
+        leave_tok(B, 1)
+        rope_tok(B, 0, 1)
+        store(B, 0, 2)
+        rope_tok(B, 1, 0)
+        rope_tok(B, 1, 1)
         store(B, 2, 4)

@@ -448,7 +448,7 @@ def tile_selfattention_pa_kernel(
             back(p3, 0)
             if k in turn:
                 sp_turn(turn[k])
-            for f, a in slot1[k]:
+            for f, a in slot1[k] + slot2[k]:
                 f(*a)
             mm(p2, 0)
             mm(p2, 1)
@@ -456,8 +456,6 @@ def tile_selfattention_pa_kernel(
             w_turn(cur, 0)
             back(p3, 1)
             store(p3)
-            for f, a in slot2[k]:
-                f(*a)
             w_quant(p1)
             leave_acc(p2, 0)
         C, B, A_, Z = SEQ[9], SEQ[8], SEQ[7], SEQ[6]

@@ -396,14 +396,14 @@ def tile_selfattention_pa_kernel(
                 in_=pb[:, a0 * P : a1 * P].rearrange("p (a h f) -> p a h f", a=a1 - a0, h=2),
             )
 
-        def store(i, a0=0, a1=A):
+        def store(i, a0=0, a1=A, queue=None):
             if i < 8:
                 dst = out_0.rearrange("(a p) o h f -> p a (o h) f", p=P)[:, :, 2 * i : 2 * i + 2, :]
             elif i == 8:
                 dst = out_1.rearrange("(a p) o h f -> p a (o h) f", p=P)
             else:
                 dst = out_2.rearrange("(a p) o h f -> p a (o h) f", p=P)
-            nc.sync.dma_start(out=dst[:, a0:a1], in_=st[("ot", i)][:, a0:a1])
+            (queue or nc.sync).dma_start(out=dst[:, a0:a1], in_=st[("ot", i)][:, a0:a1])
 
         s0, s1, s2 = SEQ[0], SEQ[1], SEQ[2]
         for c in range(G):
@@ -468,12 +468,12 @@ def tile_selfattention_pa_kernel(
         leave_acc(A_, 0)
         mm_tok(C, 1)
         w_quant(B)
-        back(Z, 0)
-        back(Z, 1)
-        store(Z)
         leave_tok(C, 0)
         rope_tok(C, 0, 0)
         mm_tok(B, 0)
+        back(Z, 0)
+        back(Z, 1)
+        store(Z, queue=nc.scalar)
         leave_tok(C, 1)
         rope_tok(C, 0, 1)
         store(C, 0, 2)
@@ -481,7 +481,7 @@ def tile_selfattention_pa_kernel(
         rope_tok(C, 1, 0)
         back(A_, 1)
         back(A_, 0)
-        store(A_)
+        store(A_, queue=nc.scalar)
         leave_tok(B, 0)
         rope_tok(C, 1, 1)
         store(C, 2, 4)

@@ -21,7 +21,6 @@ TOK = 512
 A = 4
 NPAIR = 10
 ROPE_PAIRS = 9
-MANUAL = True
 SEQ = [9, 0, 1, 2, 3, 4, 5, 6, 7, 8]
 
 
@@ -32,53 +31,54 @@ def tile_selfattention_pa_kernel(
     with ExitStack() as ctx:
         const = ctx.enter_context(tc.tile_pool(name="const", bufs=1))
         wbp = ctx.enter_context(tc.tile_pool(name="wbp", bufs=3))
-        grpp = ctx.enter_context(tc.tile_pool(name="grpp", bufs=3))
-        wqp = ctx.enter_context(tc.tile_pool(name="wqp", bufs=3))
-        mp = ctx.enter_context(tc.tile_pool(name="mp", bufs=2))
+        rawp = ctx.enter_context(tc.tile_pool(name="rawp", bufs=5))
+        grpp = ctx.enter_context(tc.tile_pool(name="grpp", bufs=4))
+        wqp = ctx.enter_context(tc.tile_pool(name="wqp", bufs=4))
+        mp = ctx.enter_context(tc.tile_pool(name="mp", bufs=3))
         ap_ = ctx.enter_context(tc.tile_pool(name="ap", bufs=3))
         otp = ctx.enter_context(tc.tile_pool(name="otp", bufs=4))
         rtp = ctx.enter_context(tc.tile_pool(name="rtp", bufs=2))
-        pfp = ctx.enter_context(tc.psum_pool(name="pfp", bufs=3))
-        accp = ctx.enter_context(tc.psum_pool(name="accp", bufs=3))
+        pfp = ctx.enter_context(tc.psum_pool(name="pfp", bufs=4))
+        accp = ctx.enter_context(tc.psum_pool(name="accp", bufs=2))
         pbp = ctx.enter_context(tc.psum_pool(name="pbp", bufs=2))
-        if MANUAL:
-            ctx.enter_context(tc.manual_schedule())
+        ctx.enter_context(tc.manual_schedule())
 
-        sc = const.tile([P, 2, K], F32, name="sc")
-        sflat = Wqkv_scale.rearrange("o k -> (o k)")
+        scol = const.tile([P, G, 4], F32, name="scol")
+        rraw = const.tile([P, A, 64], BF16, name="rraw")
+        nc.scalar.dma_start(out=rraw[:], in_=rotary_pos_emb.rearrange("(a p) o j c -> p a (o j c)", p=P))
+        nc.scalar.dma_start(out=scol[:], in_=Wqkv_scale.rearrange("o (g p t) -> p (o g) t", p=P, t=4))
+        warm = const.tile([P, 2], F32, name="warm")
+        nc.vector.memset(warm[:, 0:1], 0.0)
+        nc.scalar.activation(out=warm[:, 1:2], in_=warm[:, 0:1], func=ACT.Copy)
+
         wby = {}
         for i in SEQ:
             wbytes = const.tile([P, 2, K], U8, name="wbytes%d" % i)
             wby[i] = wbytes
 
-        def load_sc(c):
+        def load_w(i):
             nc.sync.dma_start(
-                out=sc[:, 0, c * 512 : (c + 1) * 512],
-                in_=sflat[c * 512 : (c + 1) * 512].partition_broadcast(P),
+                out=wby[i][:], in_=Wqkv_bytes[i * 256 : (i + 1) * 256, :].rearrange("(h p) k -> p h k", p=P)
             )
 
-        def load_w(i, h0, h1):
-            nc.sync.dma_start(
-                out=wby[i][:, h0:h1, :],
-                in_=Wqkv_bytes[i * 256 + h0 * P : i * 256 + h1 * P, :].rearrange("(h p) k -> p h k", p=P),
-            )
-
-        load_sc(0)
-        load_w(SEQ[0], 0, 1)
-        load_sc(1)
-        load_sc(2)
-        load_sc(3)
-        load_w(SEQ[0], 1, 2)
-        load_w(SEQ[1], 0, 2)
         xv = hidden_states.rearrange("(a p) o k -> a p (o k)", p=P)
         xraw = []
         for a in range(A):
             xr = const.tile([P, K], BF16, name="xraw%d" % a)
-            nc.sync.dma_start(out=xr[:], in_=xv[a])
             xraw.append(xr)
-        for i in SEQ[2:4]:
-            load_w(i, 0, 2)
-        load_w(SEQ[NPAIR - 1], 0, 2)
+
+        def load_x(a):
+            nc.sync.dma_start(out=xraw[a][:], in_=xv[a])
+
+        for h in range(2):
+            nc.sync.dma_start(
+                out=wby[SEQ[0]][:, h : h + 1, :],
+                in_=Wqkv_bytes[SEQ[0] * 256 + h * P : SEQ[0] * 256 + (h + 1) * P, :].rearrange("(h p) k -> p h k", p=P),
+            )
+        for a in range(A):
+            load_x(a)
+        for i in SEQ[1:3]:
+            load_w(i)
         brows = const.tile([P, P], BF16, name="brows")
         nc.gpsimd.memset(brows[:], 0.0)
         bv = bqkv.rearrange("(i h x f) -> x i h f", h=2, x=2, f=64)
@@ -87,22 +87,14 @@ def tile_selfattention_pa_kernel(
                 out=brows[x * 16 : x * 16 + NPAIR, :].rearrange("i (h f) -> i h f", h=2),
                 in_=bv[x],
             )
-        for i in SEQ[4 : NPAIR - 1]:
-            load_w(i, 0, 2)
+        for i in SEQ[3:]:
+            load_w(i)
         NAT = (SEQ[NPAIR - 2], SEQ[NPAIR - 1])
         brow = {}
         for i in NAT:
             br = const.tile([P, 256], BF16, name="brow%d" % i)
             brow[i] = br
             nc.sync.dma_start(out=br[:], in_=bqkv[i * 256 : (i + 1) * 256].partition_broadcast(P))
-        scol = const.tile([P, G, 4], F32, name="scol")
-        nc.sync.dma_start(out=scol[:], in_=Wqkv_scale.rearrange("o (g p t) -> p (o g) t", p=P, t=4))
-
-        rraw = const.tile([P, A, 64], BF16, name="rraw")
-        nc.scalar.dma_start(out=rraw[:], in_=rotary_pos_emb.rearrange("(a p) o j c -> p a (o j c)", p=P))
-        warm = const.tile([P, 2], F32, name="warm")
-        nc.vector.memset(warm[:, 0:1], 0.0)
-        nc.scalar.activation(out=warm[:, 1:2], in_=warm[:, 0:1], func=ACT.Copy)
 
         ident = const.tile([P, P], F32, name="ident")
         make_identity(nc, ident[:])
@@ -118,16 +110,16 @@ def tile_selfattention_pa_kernel(
         ttv = tt[:].rearrange("p (q a h j e) -> p q a h j e", q=2, a=A, h=2, e=2)
         rv = rraw[:].rearrange("p a (j c) -> p a j c", c=2)
         for e in range(2):
-            nc.scalar.activation(
-                out=ttv[:, 0, :, :, :, e],
-                in_=rv[:, :, :, 0].unsqueeze(2).to_broadcast([P, A, 2, 32]),
-                func=ACT.Copy,
+            nc.gpsimd.tensor_copy(
+                out=ttv[:, 0, :, :, :, e], in_=rv[:, :, :, 0].unsqueeze(2).to_broadcast([P, A, 2, 32])
             )
-            nc.scalar.activation(
+            nc.gpsimd.tensor_scalar(
                 out=ttv[:, 1, :, :, :, e],
-                in_=rv[:, :, :, 1].unsqueeze(2).to_broadcast([P, A, 2, 32]),
-                func=ACT.Copy,
-                scale=(1.0 if e == 0 else -1.0),
+                in0=rv[:, :, :, 1].unsqueeze(2).to_broadcast([P, A, 2, 32]),
+                scalar1=(1.0 if e == 0 else -1.0),
+                scalar2=0.0,
+                op0=ALU.mult,
+                op1=ALU.add,
             )
         cs = const.tile([P, 2, TOK], F32, name="cs")
 
@@ -151,28 +143,20 @@ def tile_selfattention_pa_kernel(
 
         st = {}
 
-        def transposes(words, g0, g1):
-            banks = []
-            for gb in range(g0, g1, 2):
-                ng = min(2, g1 - gb)
-                pf = pfp.tile([P, 512], F32, name="pf", tag="pf")
-                for c in range(2 * ng):
-                    g = gb + c // 2
-                    u = c % 2
-                    nc.tensor.transpose(
-                        out=pf[:, c * P : (c + 1) * P],
-                        in_=words[:, 256 * g + u : 256 * (g + 1) : 2],
-                        identity=ident[:],
-                    )
-                banks.append((pf, gb, ng))
-            return banks
-
-        def x_turn(a):
-            for pf, gb, ng in transposes(xraw[a][:].bitcast(F32), 0, G):
-                nc.scalar.copy(
-                    out=xgw[:, gb : gb + ng, a * P : (a + 1) * P, :],
-                    in_=pf[:, 0 : ng * 256].rearrange("p (g u r) -> p g r u", g=ng, u=2),
+        def x_turn(a, gb, eng):
+            words = xraw[a][:].bitcast(F32)
+            pf = pfp.tile([P, 512], F32, name="pf", tag="pf")
+            for c in range(4):
+                g, u = gb + c // 2, c % 2
+                nc.tensor.transpose(
+                    out=pf[:, c * P : (c + 1) * P],
+                    in_=words[:, 256 * g + u : 256 * (g + 1) : 2],
+                    identity=ident[:],
                 )
+            (nc.scalar.copy if eng == "s" else nc.vector.tensor_copy)(
+                out=xgw[:, gb : gb + 2, a * P : (a + 1) * P, :],
+                in_=pf[:].rearrange("p (g u r) -> p g r u", g=2, u=2),
+            )
 
         def x_quant(g0, g1):
             nc.vector.quantize_mx(
@@ -181,53 +165,76 @@ def tile_selfattention_pa_kernel(
                 in_=xg[:, g0 * TOK * 4 : g1 * TOK * 4],
             )
 
-        def sc_copy(g0, g1):
-            cols = slice(g0 * 512, g1 * 512)
-            nc.scalar.copy(out=sc[:, 1, cols], in_=sc[:, 0, cols])
-
-        def wb_tile(i):
+        def cast(i, h=None, g0=0, g1=G, eng="s"):
             if ("wb", i) not in st:
                 wb = wbp.tile([P, 2, K], BF16, name="wb", tag="wb")
                 st[("wb", i)] = wb
-            return st[("wb", i)]
+            wb = st[("wb", i)]
+            if h is None:
+                nc.scalar.copy(
+                    out=wb[:].rearrange("p h k -> p (h k)"), in_=wby[i][:].rearrange("p h k -> p (h k)").bitcast(FP8)
+                )
+            else:
+                cols = slice(g0 * 512, g1 * 512)
+                (nc.scalar.copy if eng == "s" else nc.vector.tensor_copy)(
+                    out=wb[:, h, cols], in_=wby[i][:, h, cols].bitcast(FP8)
+                )
 
-        def widen(i, h, g0=0, g1=G):
-            wb = wb_tile(i)
-            cols = slice(g0 * 512, g1 * 512)
-            nc.vector.tensor_tensor(
-                out=wb[:, h, cols], in0=wby[i][:, h, cols].bitcast(FP8), in1=sc[:, 0, cols], op=ALU.mult
-            )
+        def w_bank(i, g):
+            wb = st[("wb", i)]
+            pf = pfp.tile([P, 512], F32, name="pf", tag="pf")
+            st[("pf", i, g)] = pf
+            for h in range(2):
+                words = wb[:, h, :].bitcast(F32)
+                for u in range(2):
+                    if i in NAT:
+                        out = pf[:, (2 * u + h) * P : (2 * u + h + 1) * P]
+                        idn = ident[:]
+                    else:
+                        out = pf[:].rearrange("p (u x h f) -> p u x h f", u=2, x=2, h=2)[:, u, :, h, :]
+                        idn = ident[:].rearrange("p (x f) -> p x f", x=2)
+                    nc.tensor.matmul(
+                        out=out,
+                        lhsT=words[:, 256 * g + u : 256 * (g + 1) : 2],
+                        rhs=idn,
+                        is_transpose=True,
+                        start=True,
+                        stop=True,
+                    )
 
-        def widen2(i):
-            wb = wb_tile(i)
+        def grp_of(i):
+            if ("grp", i) not in st:
+                grp = grpp.tile([P, 2 * K], BF16, name="grp", tag="grp", align_bytes=64)
+                st[("grp", i)] = grp
+            return st[("grp", i)]
+
+        def leave_v(i, g):
+            grp = grp_of(i)
             nc.vector.tensor_tensor(
-                out=wb[:].rearrange("p h k -> p (h k)"),
-                in0=wby[i][:].rearrange("p h k -> p (h k)").bitcast(FP8),
-                in1=sc[:].rearrange("p h k -> p (h k)"),
+                out=grp[:, g * 1024 : (g + 1) * 1024].rearrange("p (n u e) -> p n u e", u=2, e=2),
+                in0=st[("pf", i, g)][:].bitcast(BF16).rearrange("p (u n e) -> p n u e", u=2, e=2),
+                in1=scol[:, g, :].rearrange("p (u e) -> p u e", u=2).unsqueeze(1).to_broadcast([P, 256, 2, 2]),
                 op=ALU.mult,
             )
 
-        def w_turn(i, h, g0=0, g1=G):
-            if h == 0 and g0 == 0:
-                grp = grpp.tile([P, 2 * K], BF16, name="grp", tag="grp", align_bytes=64)
-                st[("grp", i)] = grp
-            grp = st[("grp", i)]
-            grpw = grp[:].bitcast(F32).rearrange("p (g x h f u) -> p g x h f u", g=G, x=2, h=2, u=2)
-            grpn = grp[:].bitcast(F32).rearrange("p (g h r u) -> p g h r u", g=G, h=2, u=2)
-            for pf, gb, ng in transposes(st[("wb", i)][:, h, :].bitcast(F32), g0, g1):
-                if i in NAT:
-                    nc.scalar.copy(
-                        out=grpn[:, gb : gb + ng, h, :, :],
-                        in_=pf[:, 0 : ng * 256].rearrange("p (g u r) -> p g r u", g=ng, u=2),
-                    )
-                else:
-                    nc.scalar.copy(
-                        out=grpw[:, gb : gb + ng, :, h, :, :],
-                        in_=pf[:, 0 : ng * 256].rearrange("p (g u x f) -> p g x f u", g=ng, u=2, x=2),
-                    )
+        def leave_s(i, g):
+            raw = rawp.tile([P, 1024], BF16, name="raw", tag="raw")
+            nc.scalar.copy(
+                out=raw[:].bitcast(F32).rearrange("p (n u) -> p n u", u=2),
+                in_=st[("pf", i, g)][:].rearrange("p (u n) -> p n u", u=2),
+            )
+            grp = grp_of(i)
+            for c in range(2):
+                cols = slice(g * 1024 + c * 512, g * 1024 + (c + 1) * 512)
+                nc.gpsimd.tensor_tensor(
+                    out=grp[:, cols].rearrange("p (n t) -> p n t", t=4),
+                    in0=raw[:, c * 512 : (c + 1) * 512].rearrange("p (n t) -> p n t", t=4),
+                    in1=scol[:, g, :].unsqueeze(1).to_broadcast([P, 128, 4]),
+                    op=ALU.mult,
+                )
 
         def w_quant(i, g0=0, g1=G):
-            if g0 == 0:
+            if ("wq", i) not in st:
                 wq = wqp.tile([P, 2 * TOK], U32, name="wq", tag="wq", align_bytes=64)
                 ws = wqp.tile([P, 2 * TOK], U8, name="ws", tag="ws", align_bytes=64)
                 st[("wq", i)] = (wq, ws)
@@ -238,13 +245,10 @@ def tile_selfattention_pa_kernel(
                 in_=st[("grp", i)][:, g0 * 1024 : g1 * 1024],
             )
 
-        def mm(i, x, g0=0, g1=G, spare=False):
+        def mm(i, x, g0=0, g1=G):
             wq, ws = st[("wq", i)]
             if g0 == 0:
-                if spare:
-                    acc = pfp.tile([P, TOK], F32, name="acc2", tag="pf")
-                else:
-                    acc = accp.tile([P, TOK], F32, name="acc", tag="acc")
+                acc = accp.tile([P, TOK], F32, name="acc", tag="acc")
                 st[("acc", i, x)] = acc
             acc = st[("acc", i, x)]
             for g in range(g0, g1):
@@ -258,45 +262,6 @@ def tile_selfattention_pa_kernel(
                     start=(g == 0),
                     stop=(g == G - 1),
                 )
-
-        SP = SEQ[NPAIR - 1]
-        wc = const.tile([P, 2, K], BF16, name="wc")
-        spw = const.tile([P, G, 2, 256, 2], BF16, name="spw")
-        grp_sp = const.tile([P, 2 * K], BF16, name="grp_sp", align_bytes=64)
-        st[("grp", SP)] = grp_sp
-
-        def sp_cast(h, g0, g1):
-            cols = slice(g0 * 512, g1 * 512)
-            nc.scalar.copy(out=wc[:, h, cols], in_=wby[SP][:, h, cols].bitcast(FP8))
-
-        def sp_turn(g):
-            pf = pfp.tile([P, 512], F32, name="pf", tag="pf")
-            st[("spf", g)] = pf
-            for h in range(2):
-                for u in range(2):
-                    c = 2 * h + u
-                    nc.tensor.transpose(
-                        out=pf[:, c * P : (c + 1) * P],
-                        in_=wc[:, h, :].bitcast(F32)[:, 256 * g + u : 256 * (g + 1) : 2],
-                        identity=ident[:],
-                    )
-
-        def sp_scale(g):
-            pfb = st[("spf", g)][:].bitcast(BF16).rearrange("p (h u r e) -> p h u r e", h=2, u=2, e=2)
-            for u in range(2):
-                for e in range(2):
-                    nc.scalar.activation(
-                        out=spw[:, g, u, :, e].rearrange("p (h r) -> p h r", h=2),
-                        in_=pfb[:, :, u, :, e],
-                        func=ACT.Copy,
-                        scale=scol[:, g, 2 * u + e : 2 * u + e + 1],
-                    )
-
-        def sp_weave(g):
-            nc.scalar.copy(
-                out=grp_sp[:].bitcast(F32).rearrange("p (g c u) -> p g c u", g=G, u=2)[:, g],
-                in_=spw[:, g].rearrange("p u c e -> p u (c e)").bitcast(F32).rearrange("p u c -> p c u"),
-            )
 
         def mm_tok(i, half):
             wq, ws = st[("wq", i)]
@@ -405,90 +370,109 @@ def tile_selfattention_pa_kernel(
                 dst = out_2.rearrange("(a p) o h f -> p a (o h) f", p=P)
             (queue or nc.sync).dma_start(out=dst[:, a0:a1], in_=st[("ot", i)][:, a0:a1])
 
+
+        GP = {i: ((2, 3) if n % 2 == 0 else (3,)) for n, i in enumerate(SEQ)}
+
+        def vbank(i, j):
+            vs = [g for g in range(G) if g not in GP[i]]
+            if j < len(vs):
+                w_bank(i, vs[j])
+                leave_v(i, vs[j])
+
+        def sbank(i, j):
+            if j < len(GP[i]):
+                w_bank(i, GP[i][j])
+                leave_s(i, GP[i][j])
+
+        def at(n):
+            return SEQ[n] if 0 <= n < NPAIR else None
+
         s0, s1, s2 = SEQ[0], SEQ[1], SEQ[2]
-        for c in range(G):
-            widen(s0, 0, c, c + 1)
-        widen(s0, 1)
-        w_turn(s0, 0)
-        sc_copy(0, 2)
-        sc_copy(2, 4)
-        w_turn(s0, 1)
+        cast(s0, 0)
+        cast(s0, 1)
+        sbank(s0, 0)
+        vbank(s0, 0)
+        x_turn(0, 0, "s")
+        x_turn(0, 2, "s")
+        sbank(s0, 1)
+        vbank(s0, 1)
+        x_turn(1, 0, "s")
+        x_turn(1, 2, "s")
+        vbank(s0, 2)
+        x_turn(2, 0, "v")
+        x_turn(2, 2, "s")
+        cast(s1, 0)
+        x_turn(3, 0, "v")
+        x_turn(3, 2, "v")
+        cast(s1, 1)
+        sbank(s1, 0)
+        w_quant(s0)
+        x_quant(0, 2)
+        vbank(s1, 0)
+        vbank(s1, 1)
+        sbank(s1, 1)
+        x_quant(2, 4)
         tables_turn()
-        widen(s1, 0)
-        widen(s1, 1)
-        for a in range(A):
-            x_turn(a)
-        w_turn(s1, 0)
-        w_turn(s1, 1)
         pbias = pbp.tile([P, P], BF16, name="pbias", tag="pb")
         nc.tensor.transpose(out=pbias[:], in_=brows[:], identity=identb[:])
-        sp_cast(0, 0, 2)
-        sp_cast(1, 0, 2)
-        w_quant(s0)
-        widen2(s2)
-        x_quant(0, 2)
-        x_quant(2, 4)
         nc.vector.tensor_copy(out=bias[:], in_=pbias[:, 0:32].rearrange("p (x r) -> p x r", x=2)[:, :, 0:NPAIR])
-        mm(s0, 1, 0, 2)
-        mm(s0, 0, 0, 2)
-        mm(s0, 1, 2, 4)
-        leave_acc(s0, 1)
-        mm(s0, 0, 2, 4)
-        leave_acc(s0, 0)
-        w_turn(s2, 0)
-        w_quant(s1)
-        slot1 = {0: [(sp_scale, (0,))], 1: [(sp_scale, (1,))], 2: [(sp_cast, (0, 2, 4))], 3: [(sp_scale, (2,))], 4: [(sp_scale, (3,))], 5: []}
-        slot2 = {0: [(sp_weave, (0,))], 1: [(sp_weave, (1,))], 2: [(sp_cast, (1, 2, 4))], 3: [(sp_weave, (2,))], 4: [(sp_weave, (3,))], 5: []}
-        turn = {0: 0, 1: 1, 3: 2, 4: 3}
-        for n in range(3, NPAIR - 1):
-            cur, p1, p2, p3 = SEQ[n], SEQ[n - 1], SEQ[n - 2], SEQ[n - 3]
-            k = n - 3
-            widen2(cur)
-            w_turn(p1, 1)
-            back(p3, 0)
-            if k in turn:
-                sp_turn(turn[k])
-            for f, a in slot1[k] + slot2[k]:
-                f(*a)
-            mm(p2, 0)
-            mm(p2, 1)
-            leave_acc(p2, 1)
-            w_turn(cur, 0)
-            back(p3, 1)
-            store(p3)
-            w_quant(p1)
-            leave_acc(p2, 0)
-        C, B, A_, Z = SEQ[9], SEQ[8], SEQ[7], SEQ[6]
-        mm(A_, 0)
-        w_turn(B, 1)
-        w_quant(C)
-        mm_tok(C, 0)
-        mm(A_, 1)
-        leave_acc(A_, 1)
-        leave_acc(A_, 0)
-        mm_tok(C, 1)
+        vbank(s1, 2)
+        cast(s2)
+
+        LAST = NPAIR
+        for n in range(2, LAST):
+            cur, nxt = at(n), at(n + 1)
+            pq, pm, pb_ = at(n - 2), at(n - 2 - 1), at(n - 2 - 2)
+            if 2 == 2 and n == 2:
+                pq = None
+            vbank(cur, 0)
+            if nxt is not None:
+                cast(nxt)
+            sbank(cur, 0)
+            if pq is not None:
+                w_quant(pq)
+            vbank(cur, 1)
+            if pm is not None:
+                mm(pm, 0)
+                mm(pm, 1)
+                leave_acc(pm, 0)
+                leave_acc(pm, 1)
+            sbank(cur, 1)
+            vbank(cur, 2)
+            if pb_ is not None:
+                back(pb_, 0)
+                back(pb_, 1)
+                store(pb_)
+        C, B, A_, Z, Y = SEQ[9], SEQ[8], SEQ[7], SEQ[6], SEQ[5]
         w_quant(B)
-        leave_tok(C, 0)
-        rope_tok(C, 0, 0)
-        mm_tok(B, 0)
+        mm(A_, 0)
+        mm(A_, 1)
+        leave_acc(A_, 0)
+        leave_acc(A_, 1)
+        w_quant(C)
         back(Z, 0)
         back(Z, 1)
-        store(Z, queue=nc.scalar)
-        leave_tok(C, 1)
-        rope_tok(C, 0, 1)
-        store(C, 0, 2)
-        mm_tok(B, 1)
-        rope_tok(C, 1, 0)
-        back(A_, 1)
-        back(A_, 0)
-        store(A_, queue=nc.scalar)
+        store(Z)
+        mm_tok(B, 0)
         leave_tok(B, 0)
-        rope_tok(C, 1, 1)
-        store(C, 2, 4)
+        mm_tok(B, 1)
+        back(A_, 0)
+        back(A_, 1)
+        store(A_, queue=nc.scalar)
         rope_tok(B, 0, 0)
-        leave_tok(B, 1)
+        mm_tok(C, 0)
         rope_tok(B, 0, 1)
         store(B, 0, 2)
+        leave_tok(B, 1)
         rope_tok(B, 1, 0)
+        mm_tok(C, 1)
         rope_tok(B, 1, 1)
         store(B, 2, 4)
+        leave_tok(C, 0)
+        rope_tok(C, 0, 0)
+        rope_tok(C, 0, 1)
+        store(C, 0, 2)
+        leave_tok(C, 1)
+        rope_tok(C, 1, 0)
+        rope_tok(C, 1, 1)
+        store(C, 2, 4)

@@ -21,7 +21,8 @@ TOK = 512
 A = 4
 NPAIR = 10
 ROPE_PAIRS = 9
-SEQ = [9, 0, 1, 2, 3, 4, 5, 6, 7, 8]
+KG = 1024
+SEQ = [8, 0, 1, 2, 3, 4, 5, 6, 7, 9]
 
 
 def tile_selfattention_pa_kernel(
@@ -31,10 +32,10 @@ def tile_selfattention_pa_kernel(
     with ExitStack() as ctx:
         const = ctx.enter_context(tc.tile_pool(name="const", bufs=1))
         wbp = ctx.enter_context(tc.tile_pool(name="wbp", bufs=3))
-        rawp = ctx.enter_context(tc.tile_pool(name="rawp", bufs=5))
-        grpp = ctx.enter_context(tc.tile_pool(name="grpp", bufs=4))
-        wqp = ctx.enter_context(tc.tile_pool(name="wqp", bufs=4))
-        mp = ctx.enter_context(tc.tile_pool(name="mp", bufs=3))
+        rawp = ctx.enter_context(tc.tile_pool(name="rawp", bufs=4))
+        grpp = ctx.enter_context(tc.tile_pool(name="grpp", bufs=3))
+        wqp = ctx.enter_context(tc.tile_pool(name="wqp", bufs=3))
+        mp = ctx.enter_context(tc.tile_pool(name="mp", bufs=2))
         ap_ = ctx.enter_context(tc.tile_pool(name="ap", bufs=3))
         otp = ctx.enter_context(tc.tile_pool(name="otp", bufs=4))
         rtp = ctx.enter_context(tc.tile_pool(name="rtp", bufs=2))
@@ -75,10 +76,14 @@ def tile_selfattention_pa_kernel(
                 out=wby[SEQ[0]][:, h : h + 1, :],
                 in_=Wqkv_bytes[SEQ[0] * 256 + h * P : SEQ[0] * 256 + (h + 1) * P, :].rearrange("(h p) k -> p h k", p=P),
             )
+        load_w(SEQ[1])
+        sraw = const.tile([P, K - KG], F32, name="sraw")
+        nc.sync.dma_start(
+            out=sraw[:], in_=Wqkv_scale.rearrange("o k -> (o k)")[KG:K].partition_broadcast(P)
+        )
         for a in range(A):
             load_x(a)
-        for i in SEQ[1:3]:
-            load_w(i)
+        load_w(SEQ[2])
         brows = const.tile([P, P], BF16, name="brows")
         nc.gpsimd.memset(brows[:], 0.0)
         bv = bqkv.rearrange("(i h x f) -> x i h f", h=2, x=2, f=64)
@@ -89,7 +94,7 @@ def tile_selfattention_pa_kernel(
             )
         for i in SEQ[3:]:
             load_w(i)
-        NAT = (SEQ[NPAIR - 2], SEQ[NPAIR - 1])
+        NAT = (SEQ[NPAIR - 1],)
         brow = {}
         for i in NAT:
             br = const.tile([P, 256], BF16, name="brow%d" % i)
@@ -135,6 +140,7 @@ def tile_selfattention_pa_kernel(
                 nc.scalar.copy(out=cs[:, q, :], in_=ptab[:])
 
         bias = const.tile([P, 2, NPAIR], F32, name="bias")
+        scp = const.tile([P, K - KG], F32, name="scp")
 
         xg = const.tile([P, G * TOK * 4], BF16, name="xg", align_bytes=64)
         xgw = xg[:].bitcast(F32).rearrange("p (g n u) -> p g n u", g=G, u=2)
@@ -142,6 +148,16 @@ def tile_selfattention_pa_kernel(
         xs = const.tile([P, G * TOK], U8, name="xs", align_bytes=64)
 
         st = {}
+
+        def bias_turn():
+            pbias = pbp.tile([P, P], BF16, name="pbias", tag="pb")
+            st["pbias"] = pbias
+            nc.tensor.transpose(out=pbias[:], in_=brows[:], identity=identb[:])
+
+        def bias_copy():
+            nc.vector.tensor_copy(
+                out=bias[:], in_=st["pbias"][:, 0:32].rearrange("p (x r) -> p x r", x=2)[:, :, 0:NPAIR]
+            )
 
         def x_turn(a, gb, eng):
             words = xraw[a][:].bitcast(F32)
@@ -181,12 +197,14 @@ def tile_selfattention_pa_kernel(
                 )
 
         def w_bank(i, g):
-            wb = st[("wb", i)]
             pf = pfp.tile([P, 512], F32, name="pf", tag="pf")
             st[("pf", i, g)] = pf
             for h in range(2):
-                words = wb[:, h, :].bitcast(F32)
                 for u in range(2):
+                    if ("wp", i, g) in st:
+                        words = st[("wp", i, g)][:, h, :].bitcast(F32)[:, u * P : (u + 1) * P]
+                    else:
+                        words = st[("wb", i)][:, h, :].bitcast(F32)[:, 256 * g + u : 256 * (g + 1) : 2]
                     if i in NAT:
                         out = pf[:, (2 * u + h) * P : (2 * u + h + 1) * P]
                         idn = ident[:]
@@ -195,12 +213,29 @@ def tile_selfattention_pa_kernel(
                         idn = ident[:].rearrange("p (x f) -> p x f", x=2)
                     nc.tensor.matmul(
                         out=out,
-                        lhsT=words[:, 256 * g + u : 256 * (g + 1) : 2],
+                        lhsT=words,
                         rhs=idn,
                         is_transpose=True,
                         start=True,
                         stop=True,
                     )
+
+        def scales_sort():
+            nc.scalar.copy(
+                out=scp[:].rearrange("p (g u w e) -> p g u w e", u=2, w=P, e=2),
+                in_=sraw[:].rearrange("p (g w u e) -> p g u w e", u=2, w=P, e=2),
+            )
+
+        def scale_g(i, g):
+            wp = rawp.tile([P, 2, 512], BF16, name="wp", tag="raw")
+            st[("wp", i, g)] = wp
+            for h in range(2):
+                nc.gpsimd.tensor_tensor(
+                    out=wp[:, h, :].rearrange("p (u w e) -> p u w e", u=2, e=2),
+                    in0=st[("wb", i)][:, h, g * 512 : (g + 1) * 512].rearrange("p (w u e) -> p u w e", u=2, e=2),
+                    in1=scp[:, g * 512 - KG : (g + 1) * 512 - KG].rearrange("p (u w e) -> p u w e", u=2, e=2),
+                    op=ALU.mult,
+                )
 
         def grp_of(i):
             if ("grp", i) not in st:
@@ -218,20 +253,11 @@ def tile_selfattention_pa_kernel(
             )
 
         def leave_s(i, g):
-            raw = rawp.tile([P, 1024], BF16, name="raw", tag="raw")
+            grp = grp_of(i)
             nc.scalar.copy(
-                out=raw[:].bitcast(F32).rearrange("p (n u) -> p n u", u=2),
+                out=grp[:, g * 1024 : (g + 1) * 1024].bitcast(F32).rearrange("p (n u) -> p n u", u=2),
                 in_=st[("pf", i, g)][:].rearrange("p (u n) -> p n u", u=2),
             )
-            grp = grp_of(i)
-            for c in range(2):
-                cols = slice(g * 1024 + c * 512, g * 1024 + (c + 1) * 512)
-                nc.gpsimd.tensor_tensor(
-                    out=grp[:, cols].rearrange("p (n t) -> p n t", t=4),
-                    in0=raw[:, c * 512 : (c + 1) * 512].rearrange("p (n t) -> p n t", t=4),
-                    in1=scol[:, g, :].unsqueeze(1).to_broadcast([P, 128, 4]),
-                    op=ALU.mult,
-                )
 
         def w_quant(i, g0=0, g1=G):
             if ("wq", i) not in st:
@@ -371,13 +397,17 @@ def tile_selfattention_pa_kernel(
             (queue or nc.sync).dma_start(out=dst[:, a0:a1], in_=st[("ot", i)][:, a0:a1])
 
 
-        GP = {i: ((2, 3) if n % 2 == 0 else (3,)) for n, i in enumerate(SEQ)}
+        GP = {i: ((2, 3) if n % 2 else (3,)) for n, i in enumerate(SEQ)}
 
         def vbank(i, j):
             vs = [g for g in range(G) if g not in GP[i]]
             if j < len(vs):
                 w_bank(i, vs[j])
                 leave_v(i, vs[j])
+
+        def gscale(i):
+            for g in GP[i]:
+                scale_g(i, g)
 
         def sbank(i, j):
             if j < len(GP[i]):
@@ -388,91 +418,76 @@ def tile_selfattention_pa_kernel(
             return SEQ[n] if 0 <= n < NPAIR else None
 
         s0, s1, s2 = SEQ[0], SEQ[1], SEQ[2]
-        cast(s0, 0)
-        cast(s0, 1)
-        sbank(s0, 0)
+        cast(s0, 0, 0, 2)
+        cast(s0, 1, 0, 2, "v")
+        cast(s0, 0, 2, 4)
+        cast(s0, 1, 2, 4, "v")
+        scales_sort()
+        gscale(s0)
         vbank(s0, 0)
-        x_turn(0, 0, "s")
-        x_turn(0, 2, "s")
-        sbank(s0, 1)
         vbank(s0, 1)
+        cast(s1)
+        gscale(s1)
+        x_turn(0, 0, "s")
+        vbank(s0, 2)
+        x_turn(0, 2, "s")
+        sbank(s0, 0)
+        sbank(s0, 1)
+        vbank(s1, 0)
         x_turn(1, 0, "s")
         x_turn(1, 2, "s")
-        vbank(s0, 2)
-        x_turn(2, 0, "v")
-        x_turn(2, 2, "s")
-        cast(s1, 0)
-        x_turn(3, 0, "v")
-        x_turn(3, 2, "v")
-        cast(s1, 1)
-        sbank(s1, 0)
-        w_quant(s0)
-        x_quant(0, 2)
-        vbank(s1, 0)
         vbank(s1, 1)
-        sbank(s1, 1)
-        x_quant(2, 4)
-        tables_turn()
-        pbias = pbp.tile([P, P], BF16, name="pbias", tag="pb")
-        nc.tensor.transpose(out=pbias[:], in_=brows[:], identity=identb[:])
-        nc.vector.tensor_copy(out=bias[:], in_=pbias[:, 0:32].rearrange("p (x r) -> p x r", x=2)[:, :, 0:NPAIR])
+        x_turn(2, 0, "s")
+        x_turn(2, 2, "s")
         vbank(s1, 2)
+        x_turn(3, 0, "s")
+        x_turn(3, 2, "s")
+        w_quant(s0)
+        sbank(s1, 0)
+        sbank(s1, 1)
+        x_quant(0, 2)
+        x_quant(2, 4)
         cast(s2)
+        gscale(s2)
+        tables_turn()
+        bias_turn()
+        bias_copy()
 
-        LAST = NPAIR
-        for n in range(2, LAST):
+        for n in range(2, NPAIR):
             cur, nxt = at(n), at(n + 1)
-            pq, pm, pb_ = at(n - 2), at(n - 2 - 1), at(n - 2 - 2)
-            if 2 == 2 and n == 2:
-                pq = None
-            vbank(cur, 0)
+            p1, p2, p3 = at(n - 1), at(n - 2), at(n - 3)
             if nxt is not None:
                 cast(nxt)
-            sbank(cur, 0)
-            if pq is not None:
-                w_quant(pq)
+                gscale(nxt)
+            vbank(cur, 0)
+            w_quant(p1)
             vbank(cur, 1)
-            if pm is not None:
-                mm(pm, 0)
-                mm(pm, 1)
-                leave_acc(pm, 0)
-                leave_acc(pm, 1)
+            mm(p2, 1)
+            mm(p2, 0)
+            leave_acc(p2, 1)
+            leave_acc(p2, 0)
+            sbank(cur, 0)
             sbank(cur, 1)
             vbank(cur, 2)
-            if pb_ is not None:
-                back(pb_, 0)
-                back(pb_, 1)
-                store(pb_)
-        C, B, A_, Z, Y = SEQ[9], SEQ[8], SEQ[7], SEQ[6], SEQ[5]
-        w_quant(B)
-        mm(A_, 0)
-        mm(A_, 1)
-        leave_acc(A_, 0)
-        leave_acc(A_, 1)
+            if p3 is not None:
+                back(p3, 1)
+                back(p3, 0)
+                store(p3)
+        C, B, A_, Z = SEQ[9], SEQ[8], SEQ[7], SEQ[6]
         w_quant(C)
-        back(Z, 0)
-        back(Z, 1)
-        store(Z)
-        mm_tok(B, 0)
-        leave_tok(B, 0)
-        mm_tok(B, 1)
-        back(A_, 0)
+        mm(B, 0)
+        mm(B, 1)
+        leave_acc(B, 0)
+        leave_acc(B, 1)
         back(A_, 1)
+        back(A_, 0)
         store(A_, queue=nc.scalar)
-        rope_tok(B, 0, 0)
         mm_tok(C, 0)
-        rope_tok(B, 0, 1)
-        store(B, 0, 2)
-        leave_tok(B, 1)
-        rope_tok(B, 1, 0)
-        mm_tok(C, 1)
-        rope_tok(B, 1, 1)
-        store(B, 2, 4)
         leave_tok(C, 0)
-        rope_tok(C, 0, 0)
-        rope_tok(C, 0, 1)
         store(C, 0, 2)
+        mm_tok(C, 1)
+        back(B, 1)
+        back(B, 0)
+        store(B, queue=nc.scalar)
         leave_tok(C, 1)
-        rope_tok(C, 1, 0)
-        rope_tok(C, 1, 1)
         store(C, 2, 4)

@@ -31,8 +31,8 @@ def tile_selfattention_pa_kernel(
     nc = tc.nc
     with ExitStack() as ctx:
         const = ctx.enter_context(tc.tile_pool(name="const", bufs=1))
-        wbp = ctx.enter_context(tc.tile_pool(name="wbp", bufs=3))
-        rawp = ctx.enter_context(tc.tile_pool(name="rawp", bufs=4))
+        wbp = ctx.enter_context(tc.tile_pool(name="wbp", bufs=4))
+        rawp = ctx.enter_context(tc.tile_pool(name="rawp", bufs=6))
         grpp = ctx.enter_context(tc.tile_pool(name="grpp", bufs=3))
         wqp = ctx.enter_context(tc.tile_pool(name="wqp", bufs=3))
         mp = ctx.enter_context(tc.tile_pool(name="mp", bufs=2))
@@ -46,7 +46,6 @@ def tile_selfattention_pa_kernel(
 
         scol = const.tile([P, G, 4], F32, name="scol")
         rraw = const.tile([P, A, 64], BF16, name="rraw")
-        nc.scalar.dma_start(out=rraw[:], in_=rotary_pos_emb.rearrange("(a p) o j c -> p a (o j c)", p=P))
         nc.scalar.dma_start(out=scol[:], in_=Wqkv_scale.rearrange("o (g p t) -> p (o g) t", p=P, t=4))
         warm = const.tile([P, 2], F32, name="warm")
         nc.vector.memset(warm[:, 0:1], 0.0)
@@ -71,18 +70,22 @@ def tile_selfattention_pa_kernel(
         def load_x(a):
             nc.sync.dma_start(out=xraw[a][:], in_=xv[a])
 
-        for h in range(2):
+        for c in range(2):
+            cols = slice(c * KG, (c + 1) * KG)
             nc.sync.dma_start(
-                out=wby[SEQ[0]][:, h : h + 1, :],
-                in_=Wqkv_bytes[SEQ[0] * 256 + h * P : SEQ[0] * 256 + (h + 1) * P, :].rearrange("(h p) k -> p h k", p=P),
+                out=wby[SEQ[0]][:, :, cols],
+                in_=Wqkv_bytes[SEQ[0] * 256 : (SEQ[0] + 1) * 256, cols].rearrange("(h p) k -> p h k", p=P),
             )
         load_w(SEQ[1])
+        for a in range(2):
+            load_x(a)
         sraw = const.tile([P, K - KG], F32, name="sraw")
         nc.sync.dma_start(
             out=sraw[:], in_=Wqkv_scale.rearrange("o k -> (o k)")[KG:K].partition_broadcast(P)
         )
-        for a in range(A):
+        for a in range(2, A):
             load_x(a)
+        nc.sync.dma_start(out=rraw[:], in_=rotary_pos_emb.rearrange("(a p) o j c -> p a (o j c)", p=P))
         load_w(SEQ[2])
         brows = const.tile([P, P], BF16, name="brows")
         nc.gpsimd.memset(brows[:], 0.0)
@@ -114,21 +117,21 @@ def tile_selfattention_pa_kernel(
         tt = const.tile([P, 2 * A * P], F32, name="tt")
         ttv = tt[:].rearrange("p (q a h j e) -> p q a h j e", q=2, a=A, h=2, e=2)
         rv = rraw[:].rearrange("p a (j c) -> p a j c", c=2)
-        for e in range(2):
-            nc.gpsimd.tensor_copy(
-                out=ttv[:, 0, :, :, :, e], in_=rv[:, :, :, 0].unsqueeze(2).to_broadcast([P, A, 2, 32])
-            )
-            nc.gpsimd.tensor_scalar(
-                out=ttv[:, 1, :, :, :, e],
-                in0=rv[:, :, :, 1].unsqueeze(2).to_broadcast([P, A, 2, 32]),
-                scalar1=(1.0 if e == 0 else -1.0),
-                scalar2=0.0,
-                op0=ALU.mult,
-                op1=ALU.add,
-            )
         cs = const.tile([P, 2, TOK], F32, name="cs")
 
-        def tables_turn():
+        def tables_rows():
+            for e in range(2):
+                for q in range(2):
+                    nc.gpsimd.tensor_scalar(
+                        out=ttv[:, q, :, :, :, e],
+                        in0=rv[:, :, :, q].unsqueeze(2).to_broadcast([P, A, 2, 32]),
+                        scalar1=(-1.0 if q == 1 and e == 1 else 1.0),
+                        scalar2=0.0,
+                        op0=ALU.mult,
+                        op1=ALU.add,
+                    )
+
+        def tables_turn(eng="s"):
             for q in range(2):
                 ptab = pbp.tile([P, TOK], F32, name="ptab", tag="pb")
                 for a in range(A):
@@ -137,7 +140,7 @@ def tile_selfattention_pa_kernel(
                         in_=tt[:, (q * A + a) * P : (q * A + a + 1) * P],
                         identity=ident[:],
                     )
-                nc.scalar.copy(out=cs[:, q, :], in_=ptab[:])
+                (nc.scalar.copy if eng == "s" else nc.vector.tensor_copy)(out=cs[:, q, :], in_=ptab[:])
 
         bias = const.tile([P, 2, NPAIR], F32, name="bias")
         scp = const.tile([P, K - KG], F32, name="scp")
@@ -161,7 +164,8 @@ def tile_selfattention_pa_kernel(
 
         def x_turn(a, gb, eng):
             words = xraw[a][:].bitcast(F32)
-            pf = pfp.tile([P, 512], F32, name="pf", tag="pf")
+            pool, tag = ((accp, "acc"), (pbp, "pb"))[gb // 2]
+            pf = pool.tile([P, 512], F32, name="px", tag=tag)
             for c in range(4):
                 g, u = gb + c // 2, c % 2
                 nc.tensor.transpose(
@@ -220,8 +224,8 @@ def tile_selfattention_pa_kernel(
                         stop=True,
                     )
 
-        def scales_sort():
-            nc.scalar.copy(
+        def scales_sort(eng="s"):
+            {"s": nc.scalar.copy, "v": nc.vector.tensor_copy, "g": nc.gpsimd.tensor_copy}[eng](
                 out=scp[:].rearrange("p (g u w e) -> p g u w e", u=2, w=P, e=2),
                 in_=sraw[:].rearrange("p (g w u e) -> p g u w e", u=2, w=P, e=2),
             )
@@ -271,10 +275,11 @@ def tile_selfattention_pa_kernel(
                 in_=st[("grp", i)][:, g0 * 1024 : g1 * 1024],
             )
 
-        def mm(i, x, g0=0, g1=G):
+        def mm(i, x, g0=0, g1=G, spare=False):
             wq, ws = st[("wq", i)]
             if g0 == 0:
-                acc = accp.tile([P, TOK], F32, name="acc", tag="acc")
+                pool, tag = (pfp, "pf") if spare else (accp, "acc")
+                acc = pool.tile([P, TOK], F32, name="acc", tag=tag)
                 st[("acc", i, x)] = acc
             acc = st[("acc", i, x)]
             for g in range(g0, g1):
@@ -289,9 +294,10 @@ def tile_selfattention_pa_kernel(
                     stop=(g == G - 1),
                 )
 
-        def mm_tok(i, half):
+        def mm_tok(i, half, spare=False):
             wq, ws = st[("wq", i)]
-            acc = accp.tile([P, 2, 256], F32, name="acct", tag="acc")
+            pool, tag = (pfp, "pf") if spare else (accp, "acc")
+            acc = pool.tile([P, 2, 256], F32, name="acct", tag=tag)
             st[("acct", i, half)] = acc
             for a2 in range(2):
                 for g in range(G):
@@ -397,7 +403,7 @@ def tile_selfattention_pa_kernel(
             (queue or nc.sync).dma_start(out=dst[:, a0:a1], in_=st[("ot", i)][:, a0:a1])
 
 
-        GP = {i: ((2, 3) if n % 2 else (3,)) for n, i in enumerate(SEQ)}
+        GP = {i: (() if n == 0 else ((3,) if n < 5 else (2, 3))) for n, i in enumerate(SEQ)}
 
         def vbank(i, j):
             vs = [g for g in range(G) if g not in GP[i]]
@@ -418,21 +424,22 @@ def tile_selfattention_pa_kernel(
             return SEQ[n] if 0 <= n < NPAIR else None
 
         s0, s1, s2 = SEQ[0], SEQ[1], SEQ[2]
-        cast(s0, 0, 0, 2)
-        cast(s0, 1, 0, 2, "v")
+        cast(s0, 0, 0, 1)
+        cast(s0, 1, 0, 1, "v")
+        cast(s0, 0, 1, 2)
+        cast(s0, 1, 1, 2, "v")
         cast(s0, 0, 2, 4)
         cast(s0, 1, 2, 4, "v")
-        scales_sort()
-        gscale(s0)
         vbank(s0, 0)
         vbank(s0, 1)
-        cast(s1)
-        gscale(s1)
-        x_turn(0, 0, "s")
         vbank(s0, 2)
+        cast(s1)
+        x_turn(0, 0, "s")
+        vbank(s0, 3)
+        scales_sort()
+        gscale(s1)
+        tables_rows()
         x_turn(0, 2, "s")
-        sbank(s0, 0)
-        sbank(s0, 1)
         vbank(s1, 0)
         x_turn(1, 0, "s")
         x_turn(1, 2, "s")
@@ -444,7 +451,6 @@ def tile_selfattention_pa_kernel(
         x_turn(3, 2, "s")
         w_quant(s0)
         sbank(s1, 0)
-        sbank(s1, 1)
         x_quant(0, 2)
         x_quant(2, 4)
         cast(s2)
@@ -452,13 +458,15 @@ def tile_selfattention_pa_kernel(
         tables_turn()
         bias_turn()
         bias_copy()
+        cast(SEQ[3])
+        gscale(SEQ[3])
 
         for n in range(2, NPAIR):
             cur, nxt = at(n), at(n + 1)
             p1, p2, p3 = at(n - 1), at(n - 2), at(n - 3)
-            if nxt is not None:
-                cast(nxt)
-                gscale(nxt)
+            if n + 2 < NPAIR:
+                cast(at(n + 2))
+                gscale(at(n + 2))
             vbank(cur, 0)
             w_quant(p1)
             vbank(cur, 1)
@@ -471,23 +479,25 @@ def tile_selfattention_pa_kernel(
             vbank(cur, 2)
             if p3 is not None:
                 back(p3, 1)
+            if p3 is not None:
                 back(p3, 0)
                 store(p3)
+
         C, B, A_, Z = SEQ[9], SEQ[8], SEQ[7], SEQ[6]
+        mm(B, 1, spare=True)
+        mm(B, 0, spare=True)
         w_quant(C)
-        mm(B, 0)
-        mm(B, 1)
-        leave_acc(B, 0)
         leave_acc(B, 1)
+        leave_acc(B, 0)
         back(A_, 1)
         back(A_, 0)
         store(A_, queue=nc.scalar)
-        mm_tok(C, 0)
-        leave_tok(C, 0)
-        store(C, 0, 2)
-        mm_tok(C, 1)
+        mm_tok(C, 0, spare=True)
         back(B, 1)
         back(B, 0)
+        leave_tok(C, 0)
+        store(C, 0, 2)
+        mm_tok(C, 1, spare=True)
         store(B, queue=nc.scalar)
         leave_tok(C, 1)
         store(C, 2, 4)

@@ -77,6 +77,7 @@ def tile_selfattention_pa_kernel(
                 in_=Wqkv_bytes[SEQ[0] * 256 : (SEQ[0] + 1) * 256, cols].rearrange("(h p) k -> p h k", p=P),
             )
         load_w(SEQ[1])
+        nc.sync.dma_start(out=rraw[:], in_=rotary_pos_emb.rearrange("(a p) o j c -> p a (o j c)", p=P))
         for a in range(2):
             load_x(a)
         sraw = const.tile([P, K - KG], F32, name="sraw")
@@ -85,7 +86,6 @@ def tile_selfattention_pa_kernel(
         )
         for a in range(2, A):
             load_x(a)
-        nc.sync.dma_start(out=rraw[:], in_=rotary_pos_emb.rearrange("(a p) o j c -> p a (o j c)", p=P))
         load_w(SEQ[2])
         brows = const.tile([P, P], BF16, name="brows")
         nc.gpsimd.memset(brows[:], 0.0)
@@ -424,6 +424,7 @@ def tile_selfattention_pa_kernel(
             return SEQ[n] if 0 <= n < NPAIR else None
 
         s0, s1, s2 = SEQ[0], SEQ[1], SEQ[2]
+        tables_rows()
         cast(s0, 0, 0, 1)
         cast(s0, 1, 0, 1, "v")
         cast(s0, 0, 1, 2)
@@ -436,10 +437,9 @@ def tile_selfattention_pa_kernel(
         cast(s1)
         x_turn(0, 0, "s")
         vbank(s0, 3)
+        x_turn(0, 2, "s")
         scales_sort()
         gscale(s1)
-        tables_rows()
-        x_turn(0, 2, "s")
         vbank(s1, 0)
         x_turn(1, 0, "s")
         x_turn(1, 2, "s")

@@ -78,13 +78,7 @@ def tile_selfattention_pa_kernel(
             )
         load_w(SEQ[1])
         nc.sync.dma_start(out=rraw[:], in_=rotary_pos_emb.rearrange("(a p) o j c -> p a (o j c)", p=P))
-        for a in range(2):
-            load_x(a)
-        sraw = const.tile([P, K - KG], F32, name="sraw")
-        nc.sync.dma_start(
-            out=sraw[:], in_=Wqkv_scale.rearrange("o k -> (o k)")[KG:K].partition_broadcast(P)
-        )
-        for a in range(2, A):
+        for a in range(A):
             load_x(a)
         load_w(SEQ[2])
         brows = const.tile([P, P], BF16, name="brows")
@@ -224,10 +218,20 @@ def tile_selfattention_pa_kernel(
                         stop=True,
                     )
 
-        def scales_sort(eng="s"):
-            {"s": nc.scalar.copy, "v": nc.vector.tensor_copy, "g": nc.gpsimd.tensor_copy}[eng](
-                out=scp[:].rearrange("p (g u w e) -> p g u w e", u=2, w=P, e=2),
-                in_=sraw[:].rearrange("p (g w u e) -> p g u w e", u=2, w=P, e=2),
+        def scales_spread(g, eng="s"):
+            pz = pbp.tile([P, 512], F32, name="pz", tag="pb")
+            for t in range(4):
+                nc.tensor.matmul(
+                    out=pz[:, t * P : (t + 1) * P],
+                    lhsT=scol[:, g, t : t + 1].to_broadcast([P, P]),
+                    rhs=ident[:],
+                    is_transpose=True,
+                    start=True,
+                    stop=True,
+                )
+            (nc.scalar.copy if eng == "s" else nc.vector.tensor_copy)(
+                out=scp[:, g * 512 - KG : (g + 1) * 512 - KG].rearrange("p (u w e) -> p u w e", u=2, e=2),
+                in_=pz[:].rearrange("p (u e w) -> p u w e", u=2, e=2),
             )
 
         def scale_g(i, g):
@@ -325,14 +329,15 @@ def tile_selfattention_pa_kernel(
 
         ttq = tt[:].rearrange("p (q a h c) -> p q a h c", q=2, a=A, h=2)
 
-        def rope_tok(i, half, step):
+        def rope_tok(i, half, step, eng="v"):
+            tt_ = nc.gpsimd.tensor_tensor if eng == "g" else nc.vector.tensor_tensor
             rot = st[("ot", i)][:, 2 * half : 2 * half + 2, :, 0:64]
             if step == 0:
                 t1 = rtp.tile([P, 2, 2, 64], F32, name="t1", tag="t1")
                 m1 = rtp.tile([P, 2, 2, 64], F32, name="m1", tag="m1")
                 st[("rt", i, half)] = (t1, m1)
-                nc.vector.tensor_tensor(out=t1[:], in0=rot, in1=ttq[:, 0, 2 * half : 2 * half + 2], op=ALU.mult)
-                nc.vector.tensor_tensor(
+                tt_(out=t1[:], in0=rot, in1=ttq[:, 0, 2 * half : 2 * half + 2], op=ALU.mult)
+                tt_(
                     out=m1[:].rearrange("p a h (j e) -> p (a h) j e", e=2),
                     in0=rot.rearrange("p a h (j e) -> p (a h) j e", e=2)[:, :, :, ::-1],
                     in1=ttq[:, 1, 2 * half : 2 * half + 2].rearrange("p a h (j e) -> p (a h) j e", e=2),
@@ -340,7 +345,7 @@ def tile_selfattention_pa_kernel(
                 )
             else:
                 t1, m1 = st[("rt", i, half)]
-                nc.vector.tensor_tensor(out=rot, in0=t1[:], in1=m1[:], op=ALU.subtract)
+                tt_(out=rot, in0=t1[:], in1=m1[:], op=ALU.subtract)
 
         def is_rope(i, x):
             return x == 0 and i < ROPE_PAIRS
@@ -430,16 +435,16 @@ def tile_selfattention_pa_kernel(
         cast(s0, 0, 1, 2)
         cast(s0, 1, 1, 2, "v")
         cast(s0, 0, 2, 4)
-        cast(s0, 1, 2, 4, "v")
+        cast(s0, 1, 2, 4)
         vbank(s0, 0)
         vbank(s0, 1)
+        scales_spread(3)
         vbank(s0, 2)
-        cast(s1)
-        x_turn(0, 0, "s")
         vbank(s0, 3)
-        x_turn(0, 2, "s")
-        scales_sort()
+        cast(s1)
         gscale(s1)
+        x_turn(0, 0, "s")
+        x_turn(0, 2, "s")
         vbank(s1, 0)
         x_turn(1, 0, "s")
         x_turn(1, 2, "s")
@@ -449,6 +454,7 @@ def tile_selfattention_pa_kernel(
         vbank(s1, 2)
         x_turn(3, 0, "s")
         x_turn(3, 2, "s")
+        scales_spread(2)
         w_quant(s0)
         sbank(s1, 0)
         x_quant(0, 2)

from contextlib import ExitStack

import concourse.mybir as mybir
from concourse.masks import make_identity

FLOPS = 2 * 512 * 2560 * 2048

F32 = mybir.dt.float32
BF16 = mybir.dt.bfloat16
U32 = mybir.dt.uint32
U8 = mybir.dt.uint8
FP8 = mybir.dt.float8_e4m3fn
FP8X4 = mybir.dt.float8_e4m3fn_x4
ALU = mybir.AluOpType
ACT = mybir.ActivationFunctionType

P = 128
K = 2048
G = 4
TOK = 512
A = 4
NPAIR = 10
ROPE_PAIRS = 9
KG = 1024
SEQ = [8, 0, 1, 2, 3, 4, 5, 6, 7, 9]


def tile_selfattention_pa_kernel(
    tc, hidden_states, Wqkv_bytes, Wqkv_scale, bqkv, rotary_pos_emb, out_0, out_1, out_2
):
    nc = tc.nc
    with ExitStack() as ctx:
        const = ctx.enter_context(tc.tile_pool(name="const", bufs=1))
        wbp = ctx.enter_context(tc.tile_pool(name="wbp", bufs=4))
        rawp = ctx.enter_context(tc.tile_pool(name="rawp", bufs=6))
        grpp = ctx.enter_context(tc.tile_pool(name="grpp", bufs=3))
        wqp = ctx.enter_context(tc.tile_pool(name="wqp", bufs=3))
        mp = ctx.enter_context(tc.tile_pool(name="mp", bufs=2))
        ap_ = ctx.enter_context(tc.tile_pool(name="ap", bufs=3))
        otp = ctx.enter_context(tc.tile_pool(name="otp", bufs=4))
        rtp = ctx.enter_context(tc.tile_pool(name="rtp", bufs=2))
        pfp = ctx.enter_context(tc.psum_pool(name="pfp", bufs=4))
        accp = ctx.enter_context(tc.psum_pool(name="accp", bufs=2))
        pbp = ctx.enter_context(tc.psum_pool(name="pbp", bufs=2))
        ctx.enter_context(tc.manual_schedule())

        scol = const.tile([P, G, 4], F32, name="scol")
        rraw = const.tile([P, A, 64], BF16, name="rraw")
        nc.scalar.dma_start(out=scol[:], in_=Wqkv_scale.rearrange("o (g p t) -> p (o g) t", p=P, t=4))
        warm = const.tile([P, 2], F32, name="warm")
        nc.vector.memset(warm[:, 0:1], 0.0)
        nc.scalar.activation(out=warm[:, 1:2], in_=warm[:, 0:1], func=ACT.Copy)

        wby = {}
        for i in SEQ:
            wbytes = const.tile([P, 2, K], U8, name="wbytes%d" % i)
            wby[i] = wbytes

        def load_w(i):
            nc.sync.dma_start(
                out=wby[i][:], in_=Wqkv_bytes[i * 256 : (i + 1) * 256, :].rearrange("(h p) k -> p h k", p=P)
            )

        xv = hidden_states.rearrange("(a p) o k -> a p (o k)", p=P)
        xraw = []
        for a in range(A):
            xr = const.tile([P, K], BF16, name="xraw%d" % a)
            xraw.append(xr)

        def load_x(a):
            nc.sync.dma_start(out=xraw[a][:], in_=xv[a])

        for c in range(2):
            cols = slice(c * KG, (c + 1) * KG)
            nc.sync.dma_start(
                out=wby[SEQ[0]][:, :, cols],
                in_=Wqkv_bytes[SEQ[0] * 256 : (SEQ[0] + 1) * 256, cols].rearrange("(h p) k -> p h k", p=P),
            )
        load_w(SEQ[1])
        nc.sync.dma_start(out=rraw[:], in_=rotary_pos_emb.rearrange("(a p) o j c -> p a (o j c)", p=P))
        for a in range(A):
            load_x(a)
        load_w(SEQ[2])
        brows = const.tile([P, P], BF16, name="brows")
        nc.gpsimd.memset(brows[:], 0.0)
        bv = bqkv.rearrange("(i h x f) -> x i h f", h=2, x=2, f=64)
        for x in range(2):
            nc.sync.dma_start(
                out=brows[x * 16 : x * 16 + NPAIR, :].rearrange("i (h f) -> i h f", h=2),
                in_=bv[x],
            )
        for i in SEQ[3:]:
            load_w(i)
        NAT = (SEQ[NPAIR - 1],)
        brow = {}
        for i in NAT:
            br = const.tile([P, 256], BF16, name="brow%d" % i)
            brow[i] = br
            nc.sync.dma_start(out=br[:], in_=bqkv[i * 256 : (i + 1) * 256].partition_broadcast(P))

        ident = const.tile([P, P], F32, name="ident")
        make_identity(nc, ident[:])
        pswap = const.tile([P, P], F32, name="pswap")
        iv = ident[:].rearrange("p (j e) -> p j e", e=2)
        pv = pswap[:].rearrange("p (j e) -> p j e", e=2)
        nc.gpsimd.tensor_copy(out=pv[:, :, 0], in_=iv[:, :, 1])
        nc.gpsimd.tensor_copy(out=pv[:, :, 1], in_=iv[:, :, 0])
        identb = const.tile([P, P], BF16, name="identb")
        make_identity(nc, identb[:])

        tt = const.tile([P, 2 * A * P], F32, name="tt")
        ttv = tt[:].rearrange("p (q a h j e) -> p q a h j e", q=2, a=A, h=2, e=2)
        rv = rraw[:].rearrange("p a (j c) -> p a j c", c=2)
        cs = const.tile([P, 2, TOK], F32, name="cs")

        def tables_rows():
            for e in range(2):
                for q in range(2):
                    nc.gpsimd.tensor_scalar(
                        out=ttv[:, q, :, :, :, e],
                        in0=rv[:, :, :, q].unsqueeze(2).to_broadcast([P, A, 2, 32]),
                        scalar1=(-1.0 if q == 1 and e == 1 else 1.0),
                        scalar2=0.0,
                        op0=ALU.mult,
                        op1=ALU.add,
                    )

        def tables_turn(eng="s"):
            for q in range(2):
                ptab = pbp.tile([P, TOK], F32, name="ptab", tag="pb")
                for a in range(A):
                    nc.tensor.transpose(
                        out=ptab[:, a * P : (a + 1) * P],
                        in_=tt[:, (q * A + a) * P : (q * A + a + 1) * P],
                        identity=ident[:],
                    )
                (nc.scalar.copy if eng == "s" else nc.vector.tensor_copy)(out=cs[:, q, :], in_=ptab[:])

        bias = const.tile([P, 2, NPAIR], F32, name="bias")
        scp = const.tile([P, K - KG], F32, name="scp")

        xg = const.tile([P, G * TOK * 4], BF16, name="xg", align_bytes=64)
        xgw = xg[:].bitcast(F32).rearrange("p (g n u) -> p g n u", g=G, u=2)
        xq = const.tile([P, G * TOK], U32, name="xq", align_bytes=64)
        xs = const.tile([P, G * TOK], U8, name="xs", align_bytes=64)

        st = {}

        def bias_turn():
            pbias = pbp.tile([P, P], BF16, name="pbias", tag="pb")
            st["pbias"] = pbias
            nc.tensor.transpose(out=pbias[:], in_=brows[:], identity=identb[:])

        def bias_copy():
            nc.vector.tensor_copy(
                out=bias[:], in_=st["pbias"][:, 0:32].rearrange("p (x r) -> p x r", x=2)[:, :, 0:NPAIR]
            )

        def x_turn(a, gb, eng):
            words = xraw[a][:].bitcast(F32)
            pool, tag = ((accp, "acc"), (pbp, "pb"))[gb // 2]
            pf = pool.tile([P, 512], F32, name="px", tag=tag)
            for c in range(4):
                g, u = gb + c // 2, c % 2
                nc.tensor.transpose(
                    out=pf[:, c * P : (c + 1) * P],
                    in_=words[:, 256 * g + u : 256 * (g + 1) : 2],
                    identity=ident[:],
                )
            (nc.scalar.copy if eng == "s" else nc.vector.tensor_copy)(
                out=xgw[:, gb : gb + 2, a * P : (a + 1) * P, :],
                in_=pf[:].rearrange("p (g u r) -> p g r u", g=2, u=2),
            )

        def x_quant(g0, g1):
            nc.vector.quantize_mx(
                out=xq[:, g0 * TOK : g1 * TOK].bitcast(FP8X4),
                scales=xs[:, g0 * TOK : g1 * TOK],
                in_=xg[:, g0 * TOK * 4 : g1 * TOK * 4],
            )

        def cast(i, h=None, g0=0, g1=G, eng="s"):
            if ("wb", i) not in st:
                wb = wbp.tile([P, 2, K], BF16, name="wb", tag="wb")
                st[("wb", i)] = wb
            wb = st[("wb", i)]
            if h is None:
                nc.scalar.copy(
                    out=wb[:].rearrange("p h k -> p (h k)"), in_=wby[i][:].rearrange("p h k -> p (h k)").bitcast(FP8)
                )
            else:
                cols = slice(g0 * 512, g1 * 512)
                (nc.scalar.copy if eng == "s" else nc.vector.tensor_copy)(
                    out=wb[:, h, cols], in_=wby[i][:, h, cols].bitcast(FP8)
                )

        def w_bank(i, g):
            pf = pfp.tile([P, 512], F32, name="pf", tag="pf")
            st[("pf", i, g)] = pf
            for h in range(2):
                for u in range(2):
                    if ("wp", i, g) in st:
                        words = st[("wp", i, g)][:, h, :].bitcast(F32)[:, u * P : (u + 1) * P]
                    else:
                        words = st[("wb", i)][:, h, :].bitcast(F32)[:, 256 * g + u : 256 * (g + 1) : 2]
                    if i in NAT:
                        out = pf[:, (2 * u + h) * P : (2 * u + h + 1) * P]
                        idn = ident[:]
                    else:
                        out = pf[:].rearrange("p (u x h f) -> p u x h f", u=2, x=2, h=2)[:, u, :, h, :]
                        idn = ident[:].rearrange("p (x f) -> p x f", x=2)
                    nc.tensor.matmul(
                        out=out,
                        lhsT=words,
                        rhs=idn,
                        is_transpose=True,
                        start=True,
                        stop=True,
                    )

        def scales_spread(g, eng="s"):
            pz = pbp.tile([P, 512], F32, name="pz", tag="pb")
            for t in range(4):
                nc.tensor.matmul(
                    out=pz[:, t * P : (t + 1) * P],
                    lhsT=scol[:, g, t : t + 1].to_broadcast([P, P]),
                    rhs=ident[:],
                    is_transpose=True,
                    start=True,
                    stop=True,
                )
            (nc.scalar.copy if eng == "s" else nc.vector.tensor_copy)(
                out=scp[:, g * 512 - KG : (g + 1) * 512 - KG].rearrange("p (u w e) -> p u w e", u=2, e=2),
                in_=pz[:].rearrange("p (u e w) -> p u w e", u=2, e=2),
            )

        def scale_g(i, g):
            wp = rawp.tile([P, 2, 512], BF16, name="wp", tag="raw")
            st[("wp", i, g)] = wp
            for h in range(2):
                nc.gpsimd.tensor_tensor(
                    out=wp[:, h, :].rearrange("p (u w e) -> p u w e", u=2, e=2),
                    in0=st[("wb", i)][:, h, g * 512 : (g + 1) * 512].rearrange("p (w u e) -> p u w e", u=2, e=2),
                    in1=scp[:, g * 512 - KG : (g + 1) * 512 - KG].rearrange("p (u w e) -> p u w e", u=2, e=2),
                    op=ALU.mult,
                )

        def grp_of(i):
            if ("grp", i) not in st:
                grp = grpp.tile([P, 2 * K], BF16, name="grp", tag="grp", align_bytes=64)
                st[("grp", i)] = grp
            return st[("grp", i)]

        def leave_v(i, g):
            grp = grp_of(i)
            nc.vector.tensor_tensor(
                out=grp[:, g * 1024 : (g + 1) * 1024].rearrange("p (n u e) -> p n u e", u=2, e=2),
                in0=st[("pf", i, g)][:].bitcast(BF16).rearrange("p (u n e) -> p n u e", u=2, e=2),
                in1=scol[:, g, :].rearrange("p (u e) -> p u e", u=2).unsqueeze(1).to_broadcast([P, 256, 2, 2]),
                op=ALU.mult,
            )

        def leave_s(i, g):
            grp = grp_of(i)
            nc.scalar.copy(
                out=grp[:, g * 1024 : (g + 1) * 1024].bitcast(F32).rearrange("p (n u) -> p n u", u=2),
                in_=st[("pf", i, g)][:].rearrange("p (u n) -> p n u", u=2),
            )

        def w_quant(i, g0=0, g1=G):
            if ("wq", i) not in st:
                wq = wqp.tile([P, 2 * TOK], U32, name="wq", tag="wq", align_bytes=64)
                ws = wqp.tile([P, 2 * TOK], U8, name="ws", tag="ws", align_bytes=64)
                st[("wq", i)] = (wq, ws)
            wq, ws = st[("wq", i)]
            nc.vector.quantize_mx(
                out=wq[:, g0 * 256 : g1 * 256].bitcast(FP8X4),
                scales=ws[:, g0 * 256 : g1 * 256],
                in_=st[("grp", i)][:, g0 * 1024 : g1 * 1024],
            )

        def mm(i, x, g0=0, g1=G, spare=False):
            wq, ws = st[("wq", i)]
            if g0 == 0:
                pool, tag = (pfp, "pf") if spare else (accp, "acc")
                acc = pool.tile([P, TOK], F32, name="acc", tag=tag)
                st[("acc", i, x)] = acc
            acc = st[("acc", i, x)]
            for g in range(g0, g1):
                c0 = (g * 2 + x) * P
                nc.tensor.matmul_mx(
                    out=acc[:],
                    lhsT=wq[:, c0 : c0 + P].bitcast(FP8X4),
                    lhsT_scale=ws[:, c0 : c0 + P],
                    rhs=xq[:, g * TOK : (g + 1) * TOK].bitcast(FP8X4),
                    rhs_scale=xs[:, g * TOK : (g + 1) * TOK],
                    start=(g == 0),
                    stop=(g == G - 1),
                )

        def mm_tok(i, half, spare=False):
            wq, ws = st[("wq", i)]
            pool, tag = (pfp, "pf") if spare else (accp, "acc")
            acc = pool.tile([P, 2, 256], F32, name="acct", tag=tag)
            st[("acct", i, half)] = acc
            for a2 in range(2):
                for g in range(G):
                    c0 = g * TOK + (2 * half + a2) * P
                    nc.tensor.matmul_mx(
                        out=acc[:, a2, :],
                        lhsT=xq[:, c0 : c0 + P].bitcast(FP8X4),
                        lhsT_scale=xs[:, c0 : c0 + P],
                        rhs=wq[:, g * 256 : (g + 1) * 256].bitcast(FP8X4),
                        rhs_scale=ws[:, g * 256 : (g + 1) * 256],
                        start=(g == 0),
                        stop=(g == G - 1),
                    )

        def leave_tok(i, half):
            if ("ot", i) not in st:
                ot = otp.tile([P, A, 2, P], F32, name="ot", tag="ot")
                st[("ot", i)] = ot
            nc.vector.tensor_tensor(
                out=st[("ot", i)][:, 2 * half : 2 * half + 2, :, :].rearrange("p a h f -> p a (h f)"),
                in0=st[("acct", i, half)][:],
                in1=brow[i][:].unsqueeze(1).to_broadcast([P, 2, 256]),
                op=ALU.add,
            )

        ttq = tt[:].rearrange("p (q a h c) -> p q a h c", q=2, a=A, h=2)

        def rope_tok(i, half, step, eng="v"):
            tt_ = nc.gpsimd.tensor_tensor if eng == "g" else nc.vector.tensor_tensor
            rot = st[("ot", i)][:, 2 * half : 2 * half + 2, :, 0:64]
            if step == 0:
                t1 = rtp.tile([P, 2, 2, 64], F32, name="t1", tag="t1")
                m1 = rtp.tile([P, 2, 2, 64], F32, name="m1", tag="m1")
                st[("rt", i, half)] = (t1, m1)
                tt_(out=t1[:], in0=rot, in1=ttq[:, 0, 2 * half : 2 * half + 2], op=ALU.mult)
                tt_(
                    out=m1[:].rearrange("p a h (j e) -> p (a h) j e", e=2),
                    in0=rot.rearrange("p a h (j e) -> p (a h) j e", e=2)[:, :, :, ::-1],
                    in1=ttq[:, 1, 2 * half : 2 * half + 2].rearrange("p a h (j e) -> p (a h) j e", e=2),
                    op=ALU.mult,
                )
            else:
                t1, m1 = st[("rt", i, half)]
                tt_(out=rot, in0=t1[:], in1=m1[:], op=ALU.subtract)

        def is_rope(i, x):
            return x == 0 and i < ROPE_PAIRS

        def leave_acc(i, x, a0=0, a1=A):
            acc = st[("acc", i, x)]
            col = bias[:, x, i : i + 1]
            cols = slice(a0 * P, a1 * P)
            if is_rope(i, x):
                if a0 == 0:
                    m = mp.tile([P, 2, TOK], F32, name="m", tag="m")
                    st[("m", i, x)] = m
                m = st[("m", i, x)]
                nc.vector.scalar_tensor_tensor(
                    out=m[:, :, cols],
                    in0=acc[:, cols].unsqueeze(1).to_broadcast([P, 2, (a1 - a0) * P]),
                    scalar=col,
                    in1=cs[:, :, cols],
                    op0=ALU.add,
                    op1=ALU.mult,
                )
            else:
                av = ap_.tile([P, TOK], F32, name="av", tag="av")
                nc.scalar.activation(out=av[:], in_=acc[:], func=ACT.Identity, bias=col, scale=1.0)
                st[("m", i, x)] = av

        def back(i, x, a0=0, a1=A):
            if ("ot", i) not in st:
                ot = otp.tile([P, A, 2, P], F32, name="ot", tag="ot")
                st[("ot", i)] = ot
            ot = st[("ot", i)]
            m = st[("m", i, x)]
            if a0 == 0:
                pb = pbp.tile([P, TOK], F32, name="pb", tag="pb")
                st[("pb", i, x)] = pb
            pb = st[("pb", i, x)]
            for a in range(a0, a1):
                blk = slice(a * P, (a + 1) * P)
                if is_rope(i, x):
                    nc.tensor.matmul(
                        out=pb[:, blk], lhsT=m[:, 0, blk], rhs=ident[:], is_transpose=True, start=True, stop=False
                    )
                    nc.tensor.matmul(
                        out=pb[:, blk], lhsT=m[:, 1, blk], rhs=pswap[:], is_transpose=True, start=False, stop=True
                    )
                else:
                    nc.tensor.transpose(out=pb[:, blk], in_=m[:, blk], identity=ident[:])
            nc.scalar.copy(
                out=ot[:, a0:a1, :, x * 64 : (x + 1) * 64],
                in_=pb[:, a0 * P : a1 * P].rearrange("p (a h f) -> p a h f", a=a1 - a0, h=2),
            )

        def store(i, a0=0, a1=A, queue=None):
            if i < 8:
                dst = out_0.rearrange("(a p) o h f -> p a (o h) f", p=P)[:, :, 2 * i : 2 * i + 2, :]
            elif i == 8:
                dst = out_1.rearrange("(a p) o h f -> p a (o h) f", p=P)
            else:
                dst = out_2.rearrange("(a p) o h f -> p a (o h) f", p=P)
            (queue or nc.sync).dma_start(out=dst[:, a0:a1], in_=st[("ot", i)][:, a0:a1])


        GP = {i: (() if n == 0 else ((3,) if n < 5 else (2, 3))) for n, i in enumerate(SEQ)}

        def vbank(i, j):
            vs = [g for g in range(G) if g not in GP[i]]
            if j < len(vs):
                w_bank(i, vs[j])
                leave_v(i, vs[j])

        def gscale(i):
            for g in GP[i]:
                scale_g(i, g)

        def sbank(i, j):
            if j < len(GP[i]):
                w_bank(i, GP[i][j])
                leave_s(i, GP[i][j])

        def at(n):
            return SEQ[n] if 0 <= n < NPAIR else None

        s0, s1, s2 = SEQ[0], SEQ[1], SEQ[2]
        tables_rows()
        cast(s0, 0, 0, 1)
        cast(s0, 1, 0, 1, "v")
        cast(s0, 0, 1, 2)
        cast(s0, 1, 1, 2, "v")
        cast(s0, 0, 2, 4)
        cast(s0, 1, 2, 4)
        vbank(s0, 0)
        vbank(s0, 1)
        scales_spread(3)
        vbank(s0, 2)
        vbank(s0, 3)
        cast(s1)
        gscale(s1)
        x_turn(0, 0, "s")
        x_turn(0, 2, "s")
        vbank(s1, 0)
        x_turn(1, 0, "s")
        x_turn(1, 2, "s")
        vbank(s1, 1)
        x_turn(2, 0, "s")
        x_turn(2, 2, "s")
        vbank(s1, 2)
        x_turn(3, 0, "s")
        x_turn(3, 2, "s")
        scales_spread(2)
        w_quant(s0)
        sbank(s1, 0)
        x_quant(0, 2)
        x_quant(2, 4)
        cast(s2)
        gscale(s2)
        tables_turn()
        bias_turn()
        bias_copy()
        cast(SEQ[3])
        gscale(SEQ[3])

        for n in range(2, NPAIR):
            cur, nxt = at(n), at(n + 1)
            p1, p2, p3 = at(n - 1), at(n - 2), at(n - 3)
            if n + 2 < NPAIR:
                cast(at(n + 2))
                gscale(at(n + 2))
            vbank(cur, 0)
            w_quant(p1)
            vbank(cur, 1)
            mm(p2, 1)
            mm(p2, 0)
            leave_acc(p2, 1)
            leave_acc(p2, 0)
            sbank(cur, 0)
            sbank(cur, 1)
            vbank(cur, 2)
            if p3 is not None:
                back(p3, 1)
            if p3 is not None:
                back(p3, 0)
                store(p3)

        C, B, A_, Z = SEQ[9], SEQ[8], SEQ[7], SEQ[6]
        mm(B, 1, spare=True)
        mm(B, 0, spare=True)
        w_quant(C)
        leave_acc(B, 1)
        leave_acc(B, 0)
        back(A_, 1)
        back(A_, 0)
        store(A_, queue=nc.scalar)
        mm_tok(C, 0, spare=True)
        back(B, 1)
        back(B, 0)
        leave_tok(C, 0)
        store(C, 0, 2)
        mm_tok(C, 1, spare=True)
        store(B, queue=nc.scalar)
        leave_tok(C, 1)
        store(C, 2, 4)
